import numpy as np
import ml_dtypes


def mxq(x, axis, fmt="e4m3"):
    dtype, down = {"e4m3": (ml_dtypes.float8_e4m3fn, 7), "e5m2": (ml_dtypes.float8_e5m2, 14)}[fmt]
    v = np.moveaxis(np.asarray(x, np.float32).astype(ml_dtypes.bfloat16).astype(np.float64), axis, -1)
    blocks = v.reshape(v.shape[:-1] + (-1, 32))
    amax = np.abs(blocks).max(-1, keepdims=True)
    byte = np.maximum(np.where(amax > 0, np.frexp(amax)[1] - 1 + 127, 0) - down, 1)
    scale = np.exp2(byte - 127.0)
    codes = (blocks / scale).astype(np.float32).astype(dtype).astype(np.float64)
    return np.moveaxis((codes * scale).reshape(v.shape), -1, axis)


WIDE = False


def mx_kscale(k):
    if not WIDE:
        return np.ones(k)
    levels = np.array([10, -10, 5, -5, 0])
    if k % 512:
        return np.exp2(np.random.permutation(np.resize(levels, k // 32))).repeat(32)
    a = np.empty((k // 512, 16))
    for p in range(k // 512):
        a[p, :8] = np.random.permutation(np.resize(levels, 8))
        for g in range(8):
            far = levels[np.abs(levels - a[p, g]) >= 10]
            a[p, g + 8] = far[np.random.randint(len(far))]
    return np.exp2(a.ravel()).repeat(32)


BF16 = ml_dtypes.bfloat16


def bf(x):
    return np.asarray(x, np.float32).astype(BF16)


def f64(x):
    return np.asarray(x).astype(np.float64)


B, D, E, NM = 8192, 512, 128, 4


def setup_inputs():
    s, t = mx_kscale(D), mx_kscale(D)
    gain = np.ones((E, NM))
    gain[:, 1] = 0.3
    off = np.zeros((E, NM))
    off[:, 1] = 1.3 * np.sign(np.random.standard_normal(E))
    return {
        "prev_act": bf(np.maximum(np.random.standard_normal((B, D)) * 1.2, 0.0) * s),
        "W1": bf(np.random.standard_normal((D, D)) / np.sqrt(D) / s[:, None] * t),
        "b1": bf(np.random.standard_normal(D) * 0.2 * t),
        "W2": bf(np.random.standard_normal((D, NM * E)) / np.sqrt(D) * gain.reshape(-1) / t[:, None]),
        "b2": bf(np.random.standard_normal(NM * E) * 0.1 + off.reshape(-1)),
        "dopamine": bf(np.random.standard_normal((B, E))),
        "serotonin": bf(np.random.standard_normal((B, E))),
        "glutamate": bf(np.random.standard_normal((B, E))),
        "gaba": bf(np.random.standard_normal((B, E))),
    }


def reference(prev_act, W1, b1, W2, b2, dopamine, serotonin, glutamate, gaba):
    hid = np.maximum((mxq(f64(prev_act), 1, "e4m3") @ mxq(f64(W1), 0, "e4m3")) + f64(b1), 0.0)
    h = np.tanh((mxq(hid, 1, "e4m3") @ mxq(f64(W2), 0, "e4m3")) + f64(b2))
    preds = h.reshape(B, E, NM)
    p_dop, p_ser, p_glu, p_gab = preds[..., 0], preds[..., 1], preds[..., 2], preds[..., 3]
    inv = 1.0 / np.maximum(np.abs(p_ser), 1e-6)
    dop = f64(dopamine) + p_dop * inv
    ser = f64(serotonin) + p_ser
    glu = f64(glutamate) + p_glu * inv
    gab = f64(gaba) + p_gab * inv
    return np.concatenate([dop, ser, glu, gab], axis=0)

@@ -1,0 +1,387 @@
+from contextlib import ExitStack
+
+import concourse.mybir as mybir
+from concourse.masks import make_identity
+
+F32 = mybir.dt.float32
+BF16 = mybir.dt.bfloat16
+U32 = mybir.dt.uint32
+U8 = mybir.dt.uint8
+FP8X4 = mybir.dt.float8_e4m3fn_x4
+ACT = mybir.ActivationFunctionType
+ALU = mybir.AluOpType
+
+P = 128
+B, D, E, NM = 8192, 512, 128, 4
+FLOPS = 2 * B * D * D + 2 * B * D * NM * E
+NT = B // P
+SCT = 4
+W = SCT * P
+NSC = NT // SCT
+PAIR = 2 * SCT
+SER = 1
+OTHERS = [0, 2, 3]
+EARLY = 4
+MO_BUFS = 5
+LATE = 13
+
+
+def ser_on_scalar(i):
+    return i % 2 == 1 and i < LATE
+
+
+def back_on_scalar(i, k):
+    return i >= EARLY and (k == 2 or (k == 1 and i % 2 == 0))
+
+
+def tile_hebbianlayer_pb_t_kernel(
+    tc, prev_act, W1, b1, W2, b2, dopamine, serotonin, glutamate, gaba, out
+):
+    nc = tc.nc
+    x_view = prev_act.rearrange("(p a) k -> p (a k)", a=NT)
+    ser_view = serotonin.rearrange("(p a) j -> p a j", a=NT)
+    other_views = [m.rearrange("(p a) j -> p a j", a=NT) for m in (dopamine, glutamate, gaba)]
+    out_view = out.rearrange("(c p a) j -> p c a j", c=NM, p=P, a=NT)
+
+    with ExitStack() as ctx:
+        const = ctx.enter_context(tc.tile_pool(name="const", bufs=1))
+        xin = ctx.enter_context(tc.tile_pool(name="xin", bufs=2))
+        work = ctx.enter_context(tc.tile_pool(name="work", bufs=2))
+        codes = ctx.enter_context(tc.tile_pool(name="codes", bufs=2))
+        keep = ctx.enter_context(tc.tile_pool(name="keep", bufs=NSC))
+        serp = ctx.enter_context(tc.tile_pool(name="serp", bufs=3))
+        msp = ctx.enter_context(tc.tile_pool(name="msp", bufs=3))
+        post = ctx.enter_context(tc.tile_pool(name="post", bufs=5))
+        resp = ctx.enter_context(tc.tile_pool(name="resp", bufs=9))
+        mop = ctx.enter_context(tc.tile_pool(name="mop", bufs=MO_BUFS))
+        ps_tp = ctx.enter_context(tc.psum_pool(name="ps_tp", bufs=4))
+        ps_mm = ctx.enter_context(tc.psum_pool(name="ps_mm", bufs=4))
+        ctx.enter_context(tc.manual_schedule())
+
+        x_tiles, gx_t, xt_t, xc_t, mm_t, hidp_t, gh_t, hc_t = {}, {}, {}, {}, {}, {}, {}, {}
+        ser_t, inv_t, ht_t, ot_t, rs_t, ms_t, mo_t = {}, {}, {}, {}, {}, {}, {}
+
+        def live(i):
+            return 0 <= i < NSC
+
+        def load_x(g):
+            if g * PAIR >= NT or g in x_tiles:
+                return
+            xr = xin.tile([P, PAIR * D], BF16, name="xr")
+            pieces = 2 if g == 0 else 1
+            width = PAIR * D // pieces
+            for n in range(pieces):
+                nc.sync.dma_start(
+                    out=xr[:, n * width : (n + 1) * width],
+                    in_=x_view[:, g * PAIR * D + n * width : g * PAIR * D + (n + 1) * width],
+                )
+            x_tiles[g] = xr
+
+        def load_ser_mod(g):
+            if g < 0 or g * PAIR >= NT or g in ms_t:
+                return
+            ms = msp.tile([P, PAIR, E], BF16, name="ms")
+            nc.gpsimd.dma_start(out=ms[:], in_=ser_view[:, g * PAIR : (g + 1) * PAIR, :])
+            ms_t[g] = ms
+
+        def load_other_mods(g):
+            if g < 0 or g * PAIR >= NT or g in mo_t:
+                return
+            mo = mop.tile([P, 3, PAIR, E], BF16, name="mo")
+            for k in range(3):
+                nc.gpsimd.dma_start(out=mo[:, k, :, :], in_=other_views[k][:, g * PAIR : (g + 1) * PAIR, :])
+            mo_t[g] = mo
+
+        ident = const.tile([P, P], F32)
+        make_identity(nc, ident[:])
+        ident_bf = const.tile([P, P], BF16)
+        make_identity(nc, ident_bf[:])
+        raw1 = const.tile([P, 4, D], BF16)
+        for u in range(2):
+            nc.sync.dma_start(
+                out=raw1[:, 2 * u : 2 * u + 2, :],
+                in_=W1.rearrange("(q j) f -> q j f", j=4)[:, 2 * u : 2 * u + 2, :],
+            )
+        load_x(0)
+        b1_bf = const.tile([P, 4], BF16)
+        b2_bf = const.tile([P, 4], BF16)
+        nc.scalar.dma_start(out=b1_bf[:], in_=b1.rearrange("(m t) -> m t", t=4))
+        raw2 = const.tile([P, 4, D], BF16)
+        nc.scalar.dma_start(out=raw2[:], in_=W2.rearrange("(p t) n -> p t n", t=4))
+        nc.scalar.dma_start(out=b2_bf[:], in_=b2.rearrange("(j c) -> j c", c=4))
+        load_x(1)
+
+        g1 = const.tile([P, D, 4], BF16, align_bytes=64)
+        w1c = const.tile([P, D], U32, align_bytes=64)
+        w1s = const.tile([P, D], U8, align_bytes=64)
+        nc.vector.tensor_copy(
+            out=g1[:].rearrange("q (t m) j -> q t m j", t=4),
+            in_=raw1[:].rearrange("q j (m t) -> q t m j", t=4),
+        )
+        nc.vector.quantize_mx(
+            out=w1c[:].bitcast(FP8X4), scales=w1s[:], in_=g1[:].rearrange("q c j -> q (c j)")
+        )
+        b1t = const.tile([P, 4], F32)
+        b2t = const.tile([P, 4], F32)
+        nc.vector.tensor_copy(out=b1t[:], in_=b1_bf[:])
+        g2 = const.tile([P, D, 4], BF16, align_bytes=64)
+        w2c = const.tile([P, D], U32, align_bytes=64)
+        w2s = const.tile([P, D], U8, align_bytes=64)
+        nc.scalar.copy(
+            out=g2[:].rearrange("q (c m) j -> q c m j", c=4),
+            in_=raw2[:].rearrange("q j (m c) -> q c m j", c=4),
+        )
+
+        def quantise_w2():
+            nc.vector.tensor_copy(out=b2t[:], in_=b2_bf[:])
+            nc.vector.quantize_mx(
+                out=w2c[:].bitcast(FP8X4), scales=w2s[:], in_=g2[:].rearrange("q c j -> q (c j)")
+            )
+
+        def transpose_x(i, h):
+            if not live(i):
+                return
+            g, off = divmod(i * SCT, PAIR)
+            if off == 0 and h == 0:
+                load_x(g + 1)
+            x32 = x_tiles[g][:].bitcast(F32)
+            xt = ps_tp.tile([P, 2, 2, P], F32, name="xt", tag="tp")
+            for al in range(2):
+                for u in range(2):
+                    col = (off + 2 * h + al) * 256
+                    nc.tensor.transpose(xt[:, al, u, :], x32[:, col + u : col + 256 : 2], ident[:])
+            xt_t[(i, h)] = xt
+
+        def copy_x(i, h):
+            if not live(i):
+                return
+            if i not in gx_t:
+                gx = work.tile([P, 4 * W], BF16, align_bytes=64, name="gx")
+                gx_t[i] = gx
+            gx32 = gx_t[i][:].bitcast(F32).rearrange("q (a b u) -> q a b u", a=SCT, u=2)
+            nc.vector.tensor_copy(
+                out=gx32[:, 2 * h : 2 * h + 2], in_=xt_t[(i, h)][:].rearrange("q a u b -> q a b u")
+            )
+
+        def quantise_x(i):
+            if not live(i):
+                return
+            xc = codes.tile([P, W], U32, align_bytes=64, name="xc")
+            xs = codes.tile([P, W], U8, align_bytes=64, name="xs")
+            nc.vector.quantize_mx(out=xc[:].bitcast(FP8X4), scales=xs[:], in_=gx_t[i][:])
+            xc_t[i] = (xc, xs)
+
+        def mx_pass(key, wc, ws, col, operand):
+            acc = ps_mm.tile([P, W], F32, name="mm")
+            nc.tensor.matmul_mx(
+                out=acc[:],
+                lhsT=wc[:, col * P : (col + 1) * P].bitcast(FP8X4),
+                lhsT_scale=ws[:, col * P : (col + 1) * P],
+                rhs=operand[0][:].bitcast(FP8X4),
+                rhs_scale=operand[1][:],
+                start=True,
+                stop=True,
+            )
+            mm_t[key] = acc
+
+        def layer1(i, t):
+            if live(i):
+                mx_pass((1, i, t), w1c, w1s, t, xc_t[i])
+
+        def relu(i, t):
+            if not live(i):
+                return
+            if i not in hidp_t:
+                hidp = work.tile([P, 4, W], BF16, name="hidp")
+                hidp_t[i] = hidp
+            if i >= LATE and t >= 2:
+                nc.vector.tensor_scalar(
+                    out=hidp_t[i][:, t, :], in0=mm_t[(1, i, t)][:], scalar1=b1t[:, t : t + 1], scalar2=0.0,
+                    op0=ALU.add, op1=ALU.max,
+                )
+                return
+            nc.scalar.activation(
+                out=hidp_t[i][:, t, :], in_=mm_t[(1, i, t)][:], func=ACT.Relu, bias=b1t[:, t : t + 1], scale=1.0
+            )
+
+        def regroup_hid(i):
+            if not live(i):
+                return
+            gh = work.tile([P, W, 4], BF16, align_bytes=64, name="gh")
+            nc.vector.tensor_copy(
+                out=gh[:].rearrange("p (c i) t -> p c t i", i=4),
+                in_=hidp_t[i][:].rearrange("p t (c i) -> p c t i", i=4),
+            )
+            gh_t[i] = gh
+
+        def quantise_hid(i):
+            if not live(i):
+                return
+            hc = keep.tile([P, W], U32, align_bytes=64, name="hc")
+            hs = keep.tile([P, W], U8, align_bytes=64, name="hs")
+            nc.vector.quantize_mx(
+                out=hc[:].bitcast(FP8X4), scales=hs[:], in_=gh_t[i][:].rearrange("p w t -> p (w t)")
+            )
+            hc_t[i] = (hc, hs)
+
+        def layer2_ser(i):
+            if live(i):
+                mx_pass((2, i, SER), w2c, w2s, SER, hc_t[i])
+
+        def tanh_ser(i):
+            if not live(i):
+                return
+            ser = serp.tile([P, W], F32, name="ser")
+            nc.scalar.activation(
+                out=ser[:], in_=mm_t[(2, i, SER)][:], func=ACT.Tanh, bias=b2t[:, SER : SER + 1], scale=1.0
+            )
+            ser_t[i] = ser
+
+        def square_ser(i):
+            if not live(i):
+                return
+            inv = keep.tile([P, W], F32, name="inv")
+            nc.scalar.activation(out=inv[:], in_=ser_t[i][:], func=ACT.Square)
+            inv_t[i] = inv
+
+        def back_to_rows(key, planes, mods, on_pe):
+            bank = ps_tp.tile([P, SCT, E], F32, name="ot", tag="tp")
+            if on_pe:
+                nc.tensor.matmul(out=bank[:], lhsT=ident_bf[:], rhs=mods, start=True, stop=False)
+            for al in range(SCT):
+                src = planes[:, al * P : (al + 1) * P]
+                if on_pe:
+                    nc.tensor.matmul(
+                        out=bank[:, al, :], lhsT=src, rhs=ident[:], is_transpose=True, start=False, stop=(al == SCT - 1)
+                    )
+                else:
+                    nc.tensor.transpose(bank[:, al, :], src, ident[:])
+            ot_t[key] = bank
+
+        def leave_bank(key, mods, on_pe, rows):
+            res = resp.tile([P, SCT, E], F32, name="res")
+            if on_pe:
+                nc.scalar.copy(out=res[:], in_=ot_t[key][:])
+            else:
+                nc.vector.tensor_tensor(out=res[:], in0=ot_t[key][:], in1=mods, op=ALU.add)
+            nc.sync.dma_start(out=rows, in_=res[:])
+
+        def ser_mods(i):
+            g, off = divmod(i * SCT, PAIR)
+            return ms_t[g][:, off : off + SCT, :]
+
+        def other_mods(i, k):
+            g, off = divmod(i * SCT, PAIR)
+            return mo_t[g][:, k, off : off + SCT, :]
+
+        def transpose_ser(i):
+            if live(i):
+                back_to_rows((i, SER), ser_t[i], ser_mods(i), ser_on_scalar(i))
+
+        def exit_ser(i):
+            if live(i):
+                leave_bank((i, SER), ser_mods(i), ser_on_scalar(i), out_view[:, SER, i * SCT : (i + 1) * SCT, :])
+
+        def store_ser(i):
+            return
+
+        def layer2(i, n):
+            if live(i):
+                mx_pass((2, i, OTHERS[n]), w2c, w2s, OTHERS[n], hc_t[i])
+
+        def tanh(i, n):
+            if not live(i):
+                return
+            if i not in ht_t:
+                ht = post.tile([P, 3, W], F32, name="ht")
+                ht_t[i] = ht
+            c = OTHERS[n]
+            nc.scalar.activation(
+                out=ht_t[i][:, n, :], in_=mm_t[(2, i, c)][:], func=ACT.Tanh, bias=b2t[:, c : c + 1], scale=1.0
+            )
+
+        def products(i):
+            if not live(i):
+                return
+            nc.vector.scalar_tensor_tensor(
+                out=ht_t[i][:],
+                in0=inv_t[i][:].unsqueeze(1).to_broadcast([P, 3, W]),
+                scalar=1.0e6,
+                in1=ht_t[i][:],
+                op0=ALU.min,
+                op1=ALU.mult,
+            )
+
+        def transpose_back(i, k):
+            if live(i):
+                back_to_rows((i, OTHERS[k]), ht_t[i][:, k, :], other_mods(i, k), back_on_scalar(i, k))
+
+        def exit_back(i, k):
+            if live(i):
+                c = OTHERS[k]
+                leave_bank((i, c), other_mods(i, k), back_on_scalar(i, k), out_view[:, c, i * SCT : (i + 1) * SCT, :])
+
+        for s in range(-1, NSC + 3):
+            load_ser_mod((s - 1) // 2)
+            if s >= 2:
+                load_other_mods(min(MO_BUFS - 1, (s - 2) // 2))
+            copy_x(s, 0)
+            copy_x(s, 1)
+            square_ser(s - 3)
+            transpose_ser(s - 3)
+            transpose_x(s + 1, 0)
+            layer2_ser(s - 2)
+            if s - 13 < EARLY:
+                layer2(s - 13, 0)
+            if s - 13 < EARLY:
+                layer2(s - 13, 1)
+            if s - 13 < EARLY:
+                layer2(s - 13, 2)
+            relu(s - 1, 0)
+            relu(s - 1, 1)
+            relu(s - 1, 2)
+            relu(s - 1, 3)
+            quantise_x(s)
+            exit_ser(s - 3)
+            store_ser(s - 3)
+            tanh_ser(s - 2)
+            if s - 13 < EARLY:
+                tanh(s - 13, 0)
+            if s - 13 < EARLY:
+                tanh(s - 13, 1)
+            if s - 13 < EARLY:
+                tanh(s - 13, 2)
+            transpose_x(s + 1, 1)
+            layer1(s, 0)
+            layer1(s, 1)
+            layer1(s, 2)
+            layer1(s, 3)
+            regroup_hid(s - 1)
+            quantise_hid(s - 1)
+            if s == 0:
+                quantise_w2()
+
+        for i in range(NSC):
+            nc.scalar.activation(out=inv_t[i][:], in_=inv_t[i][:], func=ACT.Abs_reciprocal_sqrt)
+
+        for q in range(-2, NSC + 1):
+            load_other_mods((q + 8) // 2)
+            products(q)
+            transpose_back(q - 1, 0)
+            transpose_back(q - 1, 1)
+            transpose_back(q - 1, 2)
+            if q + 2 >= EARLY:
+                layer2(q + 2, 0)
+            if q + 2 >= EARLY:
+                layer2(q + 2, 1)
+            if q + 2 >= EARLY:
+                layer2(q + 2, 2)
+            exit_back(q - 1, 0)
+            exit_back(q - 1, 1)
+            exit_back(q - 1, 2)
+            if q + 2 >= EARLY:
+                tanh(q + 2, 0)
+            if q + 2 >= EARLY:
+                tanh(q + 2, 1)
+            if q + 2 >= EARLY:
+                tanh(q + 2, 2)

@@ -21,17 +21,6 @@ NSC = NT // SCT
 PAIR = 2 * SCT
 SER = 1
 OTHERS = [0, 2, 3]
-EARLY = 4
-MO_BUFS = 5
-LATE = 13
-
-
-def ser_on_scalar(i):
-    return i % 2 == 1 and i < LATE
-
-
-def back_on_scalar(i, k):
-    return i >= EARLY and (k == 2 or (k == 1 and i % 2 == 0))
 
 
 def tile_hebbianlayer_pb_t_kernel(
@@ -39,27 +28,26 @@ def tile_hebbianlayer_pb_t_kernel(
 ):
     nc = tc.nc
     x_view = prev_act.rearrange("(p a) k -> p (a k)", a=NT)
-    ser_view = serotonin.rearrange("(p a) j -> p a j", a=NT)
-    other_views = [m.rearrange("(p a) j -> p a j", a=NT) for m in (dopamine, glutamate, gaba)]
+    mod_views = [m.rearrange("(p a) j -> p a j", a=NT) for m in (dopamine, serotonin, glutamate, gaba)]
     out_view = out.rearrange("(c p a) j -> p c a j", c=NM, p=P, a=NT)
 
     with ExitStack() as ctx:
         const = ctx.enter_context(tc.tile_pool(name="const", bufs=1))
-        xin = ctx.enter_context(tc.tile_pool(name="xin", bufs=2))
+        xin = ctx.enter_context(tc.tile_pool(name="xin", bufs=3))
         work = ctx.enter_context(tc.tile_pool(name="work", bufs=2))
         codes = ctx.enter_context(tc.tile_pool(name="codes", bufs=2))
-        keep = ctx.enter_context(tc.tile_pool(name="keep", bufs=NSC))
         serp = ctx.enter_context(tc.tile_pool(name="serp", bufs=3))
-        msp = ctx.enter_context(tc.tile_pool(name="msp", bufs=3))
-        post = ctx.enter_context(tc.tile_pool(name="post", bufs=5))
-        resp = ctx.enter_context(tc.tile_pool(name="resp", bufs=9))
-        mop = ctx.enter_context(tc.tile_pool(name="mop", bufs=MO_BUFS))
+        invp = ctx.enter_context(tc.tile_pool(name="invp", bufs=3))
+        modp = ctx.enter_context(tc.tile_pool(name="modp", bufs=4))
+        post = ctx.enter_context(tc.tile_pool(name="post", bufs=4))
+        resp = ctx.enter_context(tc.tile_pool(name="resp", bufs=4))
+        sres = ctx.enter_context(tc.tile_pool(name="sres", bufs=4))
         ps_tp = ctx.enter_context(tc.psum_pool(name="ps_tp", bufs=4))
         ps_mm = ctx.enter_context(tc.psum_pool(name="ps_mm", bufs=4))
         ctx.enter_context(tc.manual_schedule())
 
         x_tiles, gx_t, xt_t, xc_t, mm_t, hidp_t, gh_t, hc_t = {}, {}, {}, {}, {}, {}, {}, {}
-        ser_t, inv_t, ht_t, ot_t, rs_t, ms_t, mo_t = {}, {}, {}, {}, {}, {}, {}
+        ser_t, inv_t, ht_t, ot_t, rs_t, mod_t = {}, {}, {}, {}, {}, {}
 
         def live(i):
             return 0 <= i < NSC
@@ -77,25 +65,16 @@ def tile_hebbianlayer_pb_t_kernel(
                 )
             x_tiles[g] = xr
 
-        def load_ser_mod(g):
-            if g < 0 or g * PAIR >= NT or g in ms_t:
+        def load_mods(g):
+            if g < 0 or g * PAIR >= NT or g in mod_t:
                 return
-            ms = msp.tile([P, PAIR, E], BF16, name="ms")
-            nc.gpsimd.dma_start(out=ms[:], in_=ser_view[:, g * PAIR : (g + 1) * PAIR, :])
-            ms_t[g] = ms
-
-        def load_other_mods(g):
-            if g < 0 or g * PAIR >= NT or g in mo_t:
-                return
-            mo = mop.tile([P, 3, PAIR, E], BF16, name="mo")
-            for k in range(3):
-                nc.gpsimd.dma_start(out=mo[:, k, :, :], in_=other_views[k][:, g * PAIR : (g + 1) * PAIR, :])
-            mo_t[g] = mo
+            mo = modp.tile([P, NM, PAIR, E], BF16, name="mo")
+            for c in [SER] + OTHERS:
+                nc.sync.dma_start(out=mo[:, c, :, :], in_=mod_views[c][:, g * PAIR : (g + 1) * PAIR, :])
+            mod_t[g] = mo
 
         ident = const.tile([P, P], F32)
         make_identity(nc, ident[:])
-        ident_bf = const.tile([P, P], BF16)
-        make_identity(nc, ident_bf[:])
         raw1 = const.tile([P, 4, D], BF16)
         for u in range(2):
             nc.sync.dma_start(
@@ -142,8 +121,6 @@ def tile_hebbianlayer_pb_t_kernel(
             if not live(i):
                 return
             g, off = divmod(i * SCT, PAIR)
-            if off == 0 and h == 0:
-                load_x(g + 1)
             x32 = x_tiles[g][:].bitcast(F32)
             xt = ps_tp.tile([P, 2, 2, P], F32, name="xt", tag="tp")
             for al in range(2):
@@ -159,9 +136,12 @@ def tile_hebbianlayer_pb_t_kernel(
                 gx = work.tile([P, 4 * W], BF16, align_bytes=64, name="gx")
                 gx_t[i] = gx
             gx32 = gx_t[i][:].bitcast(F32).rearrange("q (a b u) -> q a b u", a=SCT, u=2)
-            nc.vector.tensor_copy(
-                out=gx32[:, 2 * h : 2 * h + 2], in_=xt_t[(i, h)][:].rearrange("q a u b -> q a b u")
-            )
+            o = gx32[:, 2 * h : 2 * h + 2]
+            src = xt_t[(i, h)][:].rearrange("q a u b -> q a b u")
+            if h == 1 and i > 0:
+                nc.scalar.copy(out=o, in_=src)
+            else:
+                nc.vector.tensor_copy(out=o, in_=src)
 
         def quantise_x(i):
             if not live(i):
@@ -184,25 +164,20 @@ def tile_hebbianlayer_pb_t_kernel(
             )
             mm_t[key] = acc
 
-        def layer1(i, t):
+        def layer1(i):
             if live(i):
-                mx_pass((1, i, t), w1c, w1s, t, xc_t[i])
+                for t in range(4):
+                    mx_pass((1, i, t), w1c, w1s, t, xc_t[i])
 
-        def relu(i, t):
+        def relu(i):
             if not live(i):
                 return
-            if i not in hidp_t:
-                hidp = work.tile([P, 4, W], BF16, name="hidp")
-                hidp_t[i] = hidp
-            if i >= LATE and t >= 2:
-                nc.vector.tensor_scalar(
-                    out=hidp_t[i][:, t, :], in0=mm_t[(1, i, t)][:], scalar1=b1t[:, t : t + 1], scalar2=0.0,
-                    op0=ALU.add, op1=ALU.max,
+            hidp = work.tile([P, 4, W], BF16, name="hidp")
+            hidp_t[i] = hidp
+            for t in range(4):
+                nc.scalar.activation(
+                    out=hidp[:, t, :], in_=mm_t[(1, i, t)][:], func=ACT.Relu, bias=b1t[:, t : t + 1], scale=1.0
                 )
-                return
-            nc.scalar.activation(
-                out=hidp_t[i][:, t, :], in_=mm_t[(1, i, t)][:], func=ACT.Relu, bias=b1t[:, t : t + 1], scale=1.0
-            )
 
         def regroup_hid(i):
             if not live(i):
@@ -217,16 +192,17 @@ def tile_hebbianlayer_pb_t_kernel(
         def quantise_hid(i):
             if not live(i):
                 return
-            hc = keep.tile([P, W], U32, align_bytes=64, name="hc")
-            hs = keep.tile([P, W], U8, align_bytes=64, name="hs")
+            hc = codes.tile([P, W], U32, align_bytes=64, name="hc")
+            hs = codes.tile([P, W], U8, align_bytes=64, name="hs")
             nc.vector.quantize_mx(
                 out=hc[:].bitcast(FP8X4), scales=hs[:], in_=gh_t[i][:].rearrange("p w t -> p (w t)")
             )
             hc_t[i] = (hc, hs)
 
-        def layer2_ser(i):
+        def layer2(i):
             if live(i):
-                mx_pass((2, i, SER), w2c, w2s, SER, hc_t[i])
+                for c in [SER] + OTHERS:
+                    mx_pass((2, i, c), w2c, w2s, c, hc_t[i])
 
         def tanh_ser(i):
             if not live(i):
@@ -236,58 +212,6 @@ def tile_hebbianlayer_pb_t_kernel(
                 out=ser[:], in_=mm_t[(2, i, SER)][:], func=ACT.Tanh, bias=b2t[:, SER : SER + 1], scale=1.0
             )
             ser_t[i] = ser
-
-        def square_ser(i):
-            if not live(i):
-                return
-            inv = keep.tile([P, W], F32, name="inv")
-            nc.scalar.activation(out=inv[:], in_=ser_t[i][:], func=ACT.Square)
-            inv_t[i] = inv
-
-        def back_to_rows(key, planes, mods, on_pe):
-            bank = ps_tp.tile([P, SCT, E], F32, name="ot", tag="tp")
-            if on_pe:
-                nc.tensor.matmul(out=bank[:], lhsT=ident_bf[:], rhs=mods, start=True, stop=False)
-            for al in range(SCT):
-                src = planes[:, al * P : (al + 1) * P]
-                if on_pe:
-                    nc.tensor.matmul(
-                        out=bank[:, al, :], lhsT=src, rhs=ident[:], is_transpose=True, start=False, stop=(al == SCT - 1)
-                    )
-                else:
-                    nc.tensor.transpose(bank[:, al, :], src, ident[:])
-            ot_t[key] = bank
-
-        def leave_bank(key, mods, on_pe, rows):
-            res = resp.tile([P, SCT, E], F32, name="res")
-            if on_pe:
-                nc.scalar.copy(out=res[:], in_=ot_t[key][:])
-            else:
-                nc.vector.tensor_tensor(out=res[:], in0=ot_t[key][:], in1=mods, op=ALU.add)
-            nc.sync.dma_start(out=rows, in_=res[:])
-
-        def ser_mods(i):
-            g, off = divmod(i * SCT, PAIR)
-            return ms_t[g][:, off : off + SCT, :]
-
-        def other_mods(i, k):
-            g, off = divmod(i * SCT, PAIR)
-            return mo_t[g][:, k, off : off + SCT, :]
-
-        def transpose_ser(i):
-            if live(i):
-                back_to_rows((i, SER), ser_t[i], ser_mods(i), ser_on_scalar(i))
-
-        def exit_ser(i):
-            if live(i):
-                leave_bank((i, SER), ser_mods(i), ser_on_scalar(i), out_view[:, SER, i * SCT : (i + 1) * SCT, :])
-
-        def store_ser(i):
-            return
-
-        def layer2(i, n):
-            if live(i):
-                mx_pass((2, i, OTHERS[n]), w2c, w2s, OTHERS[n], hc_t[i])
 
         def tanh(i, n):
             if not live(i):
@@ -300,88 +224,93 @@ def tile_hebbianlayer_pb_t_kernel(
                 out=ht_t[i][:, n, :], in_=mm_t[(2, i, c)][:], func=ACT.Tanh, bias=b2t[:, c : c + 1], scale=1.0
             )
 
-        def products(i):
+        def back_to_rows(key, plane):
+            bank = ps_tp.tile([P, SCT, E], F32, name="ot", tag="tp")
+            for al in range(SCT):
+                nc.tensor.transpose(bank[:, al, :], plane[:, al * P : (al + 1) * P], ident[:])
+            ot_t[key] = bank
+
+        def mods(i, c):
+            g, off = divmod(i * SCT, PAIR)
+            return mod_t[g][:, c, off : off + SCT, :]
+
+        def store(i, c, rows):
+            nc.sync.dma_start(out=out_view[:, c, i * SCT : (i + 1) * SCT, :], in_=rows)
+
+        def transpose_ser(i):
+            if live(i):
+                back_to_rows((i, SER), ser_t[i])
+
+        def reciprocal_ser(i):
             if not live(i):
                 return
+            inv = invp.tile([P, SCT, E], F32, name="inv")
+            nc.vector.reciprocal(out=inv[:], in_=ot_t[(i, SER)][:])
+            inv_t[i] = inv
+
+        def abs_inv(i):
+            if live(i):
+                nc.scalar.activation(out=inv_t[i][:], in_=inv_t[i][:], func=ACT.Abs)
+
+        def exit_ser(i):
+            if not live(i):
+                return
+            res = sres.tile([P, SCT, E], F32, name="res")
+            nc.vector.tensor_tensor(out=res[:], in0=ot_t[(i, SER)][:], in1=mods(i, SER), op=ALU.add)
+            store(i, SER, res[:])
+
+        def transpose_others(i):
+            if live(i):
+                for n in range(3):
+                    back_to_rows((i, n), ht_t[i][:, n, :])
+
+        def products(i, n):
+            if not live(i):
+                return
+            if i not in rs_t:
+                rs = resp.tile([P, 3, SCT, E], F32, name="rs")
+                rs_t[i] = rs
             nc.vector.scalar_tensor_tensor(
-                out=ht_t[i][:],
-                in0=inv_t[i][:].unsqueeze(1).to_broadcast([P, 3, W]),
+                out=rs_t[i][:, n],
+                in0=inv_t[i][:],
                 scalar=1.0e6,
-                in1=ht_t[i][:],
+                in1=ot_t[(i, n)][:],
                 op0=ALU.min,
                 op1=ALU.mult,
             )
 
-        def transpose_back(i, k):
-            if live(i):
-                back_to_rows((i, OTHERS[k]), ht_t[i][:, k, :], other_mods(i, k), back_on_scalar(i, k))
+        def add_mods(i, n):
+            if not live(i):
+                return
+            c = OTHERS[n]
+            nc.gpsimd.tensor_tensor(out=rs_t[i][:, n], in0=rs_t[i][:, n], in1=mods(i, c), op=ALU.add)
+            store(i, c, rs_t[i][:, n])
 
-        def exit_back(i, k):
-            if live(i):
-                c = OTHERS[k]
-                leave_bank((i, c), other_mods(i, k), back_on_scalar(i, k), out_view[:, c, i * SCT : (i + 1) * SCT, :])
-
-        for s in range(-1, NSC + 3):
-            load_ser_mod((s - 1) // 2)
-            if s >= 2:
-                load_other_mods(min(MO_BUFS - 1, (s - 2) // 2))
-            copy_x(s, 0)
-            copy_x(s, 1)
-            square_ser(s - 3)
-            transpose_ser(s - 3)
-            transpose_x(s + 1, 0)
-            layer2_ser(s - 2)
-            if s - 13 < EARLY:
-                layer2(s - 13, 0)
-            if s - 13 < EARLY:
-                layer2(s - 13, 1)
-            if s - 13 < EARLY:
-                layer2(s - 13, 2)
-            relu(s - 1, 0)
-            relu(s - 1, 1)
-            relu(s - 1, 2)
-            relu(s - 1, 3)
-            quantise_x(s)
-            exit_ser(s - 3)
-            store_ser(s - 3)
-            tanh_ser(s - 2)
-            if s - 13 < EARLY:
-                tanh(s - 13, 0)
-            if s - 13 < EARLY:
-                tanh(s - 13, 1)
-            if s - 13 < EARLY:
-                tanh(s - 13, 2)
-            transpose_x(s + 1, 1)
-            layer1(s, 0)
-            layer1(s, 1)
-            layer1(s, 2)
-            layer1(s, 3)
-            regroup_hid(s - 1)
-            quantise_hid(s - 1)
-            if s == 0:
+        for p in range(-2, NSC + 4):
+            if p % 2 == 0:
+                load_x((p + 4) // 2)
+                load_mods(p // 2)
+            for n in range(3):
+                products(p - 3, n)
+                add_mods(p - 3, n)
+            transpose_x(p + 1, 0)
+            transpose_x(p + 1, 1)
+            transpose_ser(p - 2)
+            relu(p)
+            copy_x(p + 1, 0)
+            copy_x(p + 1, 1)
+            layer2(p - 1)
+            reciprocal_ser(p - 2)
+            exit_ser(p - 2)
+            tanh_ser(p - 1)
+            tanh(p - 1, 0)
+            abs_inv(p - 2)
+            tanh(p - 1, 1)
+            tanh(p - 1, 2)
+            quantise_x(p + 1)
+            regroup_hid(p)
+            quantise_hid(p)
+            transpose_others(p - 2)
+            layer1(p + 1)
+            if p == -1:
                 quantise_w2()
-
-        for i in range(NSC):
-            nc.scalar.activation(out=inv_t[i][:], in_=inv_t[i][:], func=ACT.Abs_reciprocal_sqrt)
-
-        for q in range(-2, NSC + 1):
-            load_other_mods((q + 8) // 2)
-            products(q)
-            transpose_back(q - 1, 0)
-            transpose_back(q - 1, 1)
-            transpose_back(q - 1, 2)
-            if q + 2 >= EARLY:
-                layer2(q + 2, 0)
-            if q + 2 >= EARLY:
-                layer2(q + 2, 1)
-            if q + 2 >= EARLY:
-                layer2(q + 2, 2)
-            exit_back(q - 1, 0)
-            exit_back(q - 1, 1)
-            exit_back(q - 1, 2)
-            if q + 2 >= EARLY:
-                tanh(q + 2, 0)
-            if q + 2 >= EARLY:
-                tanh(q + 2, 1)
-            if q + 2 >= EARLY:
-                tanh(q + 2, 2)

@@ -21,6 +21,21 @@ NSC = NT // SCT
 PAIR = 2 * SCT
 SER = 1
 OTHERS = [0, 2, 3]
+EARLY = 4
+EARLY_START = 3
+LAST_SER = 6
+LAST_INV = 10
+AHEAD = 3
+GW = 0
+MO_BUFS = 5
+
+
+def on_gpsimd(i, n):
+    return n < 2 and not (n == 1 and i % 4 == 3)
+
+
+def x_on_scalar(i, h):
+    return False
 
 
 def tile_hebbianlayer_pb_t_kernel(
@@ -33,21 +48,22 @@ def tile_hebbianlayer_pb_t_kernel(
 
     with ExitStack() as ctx:
         const = ctx.enter_context(tc.tile_pool(name="const", bufs=1))
-        xin = ctx.enter_context(tc.tile_pool(name="xin", bufs=3))
+        xin = ctx.enter_context(tc.tile_pool(name="xin", bufs=2))
         work = ctx.enter_context(tc.tile_pool(name="work", bufs=2))
         codes = ctx.enter_context(tc.tile_pool(name="codes", bufs=2))
         serp = ctx.enter_context(tc.tile_pool(name="serp", bufs=3))
-        invp = ctx.enter_context(tc.tile_pool(name="invp", bufs=3))
-        modp = ctx.enter_context(tc.tile_pool(name="modp", bufs=4))
-        post = ctx.enter_context(tc.tile_pool(name="post", bufs=4))
-        resp = ctx.enter_context(tc.tile_pool(name="resp", bufs=4))
+        keep = ctx.enter_context(tc.tile_pool(name="keep", bufs=NSC))
+        msp = ctx.enter_context(tc.tile_pool(name="msp", bufs=3))
+        mop = ctx.enter_context(tc.tile_pool(name="mop", bufs=MO_BUFS))
+        post = ctx.enter_context(tc.tile_pool(name="post", bufs=max(AHEAD + 1, EARLY) + 1))
+        resp = ctx.enter_context(tc.tile_pool(name="resp", bufs=3))
         sres = ctx.enter_context(tc.tile_pool(name="sres", bufs=4))
         ps_tp = ctx.enter_context(tc.psum_pool(name="ps_tp", bufs=4))
         ps_mm = ctx.enter_context(tc.psum_pool(name="ps_mm", bufs=4))
         ctx.enter_context(tc.manual_schedule())
 
         x_tiles, gx_t, xt_t, xc_t, mm_t, hidp_t, gh_t, hc_t = {}, {}, {}, {}, {}, {}, {}, {}
-        ser_t, inv_t, ht_t, ot_t, rs_t, mod_t = {}, {}, {}, {}, {}, {}
+        ser_t, inv_t, ht_t, ot_t, rs_t, ms_t, mo_t = {}, {}, {}, {}, {}, {}, {}
 
         def live(i):
             return 0 <= i < NSC
@@ -56,60 +72,77 @@ def tile_hebbianlayer_pb_t_kernel(
             if g * PAIR >= NT or g in x_tiles:
                 return
             xr = xin.tile([P, PAIR * D], BF16, name="xr")
-            pieces = 2 if g == 0 else 1
-            width = PAIR * D // pieces
-            for n in range(pieces):
-                nc.sync.dma_start(
-                    out=xr[:, n * width : (n + 1) * width],
-                    in_=x_view[:, g * PAIR * D + n * width : g * PAIR * D + (n + 1) * width],
-                )
             x_tiles[g] = xr
+            if g > 0:
+                load_x_tiles(g, 0, PAIR)
 
-        def load_mods(g):
-            if g < 0 or g * PAIR >= NT or g in mod_t:
+        def load_x_tiles(g, a, b):
+            nc.sync.dma_start(
+                out=x_tiles[g][:, a * D : b * D],
+                in_=x_view[:, (g * PAIR + a) * D : (g * PAIR + b) * D],
+            )
+
+        def load_ser_mod(g):
+            if g < 0 or g * PAIR >= NT or g in ms_t:
                 return
-            mo = modp.tile([P, NM, PAIR, E], BF16, name="mo")
-            for c in [SER] + OTHERS:
-                nc.sync.dma_start(out=mo[:, c, :, :], in_=mod_views[c][:, g * PAIR : (g + 1) * PAIR, :])
-            mod_t[g] = mo
+            ms = msp.tile([P, PAIR, E], BF16, name="ms")
+            nc.sync.dma_start(out=ms[:], in_=mod_views[SER][:, g * PAIR : (g + 1) * PAIR, :])
+            ms_t[g] = ms
+
+        def load_other_mods(g):
+            if g < 0 or g * PAIR >= NT or g in mo_t:
+                return
+            mo = mop.tile([P, 3, PAIR, E], BF16, name="mo")
+            for n in range(3):
+                nc.sync.dma_start(out=mo[:, n, :, :], in_=mod_views[OTHERS[n]][:, g * PAIR : (g + 1) * PAIR, :])
+            mo_t[g] = mo
 
         ident = const.tile([P, P], F32)
         make_identity(nc, ident[:])
+        load_x(0)
+        load_x_tiles(0, 0, 2)
         raw1 = const.tile([P, 4, D], BF16)
         for u in range(2):
             nc.sync.dma_start(
                 out=raw1[:, 2 * u : 2 * u + 2, :],
                 in_=W1.rearrange("(q j) f -> q j f", j=4)[:, 2 * u : 2 * u + 2, :],
             )
-        load_x(0)
+        load_x_tiles(0, 2, 4)
         b1_bf = const.tile([P, 4], BF16)
         b2_bf = const.tile([P, 4], BF16)
         nc.scalar.dma_start(out=b1_bf[:], in_=b1.rearrange("(m t) -> m t", t=4))
-        raw2 = const.tile([P, 4, D], BF16)
-        nc.scalar.dma_start(out=raw2[:], in_=W2.rearrange("(p t) n -> p t n", t=4))
         nc.scalar.dma_start(out=b2_bf[:], in_=b2.rearrange("(j c) -> j c", c=4))
+        load_x_tiles(0, 4, 8)
+        raw2 = const.tile([P, 4, D], BF16)
+        nc.sync.dma_start(out=raw2[:], in_=W2.rearrange("(p t) n -> p t n", t=4))
         load_x(1)
 
         g1 = const.tile([P, D, 4], BF16, align_bytes=64)
         w1c = const.tile([P, D], U32, align_bytes=64)
         w1s = const.tile([P, D], U8, align_bytes=64)
-        nc.vector.tensor_copy(
-            out=g1[:].rearrange("q (t m) j -> q t m j", t=4),
-            in_=raw1[:].rearrange("q j (m t) -> q t m j", t=4),
-        )
-        nc.vector.quantize_mx(
-            out=w1c[:].bitcast(FP8X4), scales=w1s[:], in_=g1[:].rearrange("q c j -> q (c j)")
-        )
         b1t = const.tile([P, 4], F32)
         b2t = const.tile([P, 4], F32)
-        nc.vector.tensor_copy(out=b1t[:], in_=b1_bf[:])
         g2 = const.tile([P, D, 4], BF16, align_bytes=64)
         w2c = const.tile([P, D], U32, align_bytes=64)
         w2s = const.tile([P, D], U8, align_bytes=64)
-        nc.scalar.copy(
-            out=g2[:].rearrange("q (c m) j -> q c m j", c=4),
-            in_=raw2[:].rearrange("q j (m c) -> q c m j", c=4),
-        )
+
+        def regroup_w1(copy, half):
+            copy(
+                out=g1[:].rearrange("q (t m) j -> q t m j", t=4)[:, 2 * half : 2 * half + 2],
+                in_=raw1[:].rearrange("q j (m t) -> q t m j", t=4)[:, 2 * half : 2 * half + 2],
+            )
+
+        def quantise_w1(half):
+            cols = slice(half * D // 2, (half + 1) * D // 2)
+            nc.vector.quantize_mx(
+                out=w1c[:, cols].bitcast(FP8X4), scales=w1s[:, cols], in_=g1[:, cols, :].rearrange("q c j -> q (c j)")
+            )
+
+        def regroup_w2():
+            nc.scalar.copy(
+                out=g2[:].rearrange("q (c m) j -> q c m j", c=4),
+                in_=raw2[:].rearrange("q j (m c) -> q c m j", c=4),
+            )
 
         def quantise_w2():
             nc.vector.tensor_copy(out=b2t[:], in_=b2_bf[:])
@@ -138,7 +171,7 @@ def tile_hebbianlayer_pb_t_kernel(
             gx32 = gx_t[i][:].bitcast(F32).rearrange("q (a b u) -> q a b u", a=SCT, u=2)
             o = gx32[:, 2 * h : 2 * h + 2]
             src = xt_t[(i, h)][:].rearrange("q a u b -> q a b u")
-            if h == 1 and i > 0:
+            if x_on_scalar(i, h):
                 nc.scalar.copy(out=o, in_=src)
             else:
                 nc.vector.tensor_copy(out=o, in_=src)
@@ -183,26 +216,32 @@ def tile_hebbianlayer_pb_t_kernel(
             if not live(i):
                 return
             gh = work.tile([P, W, 4], BF16, align_bytes=64, name="gh")
-            nc.vector.tensor_copy(
-                out=gh[:].rearrange("p (c i) t -> p c t i", i=4),
-                in_=hidp_t[i][:].rearrange("p t (c i) -> p c t i", i=4),
-            )
             gh_t[i] = gh
+            vw = W - (GW if 0 < i else 0)
+            nc.vector.tensor_copy(
+                out=gh[:, :vw].rearrange("p (c i) t -> p c t i", i=4),
+                in_=hidp_t[i][:, :, :vw].rearrange("p t (c i) -> p c t i", i=4),
+            )
+            if vw < W:
+                nc.gpsimd.tensor_scalar(
+                    out=gh[:, vw:].rearrange("p (c i) t -> p c t i", i=4),
+                    in0=hidp_t[i][:, :, vw:].rearrange("p t (c i) -> p c t i", i=4),
+                    scalar1=1.0, scalar2=0.0, op0=ALU.mult, op1=ALU.add,
+                )
 
         def quantise_hid(i):
             if not live(i):
                 return
-            hc = codes.tile([P, W], U32, align_bytes=64, name="hc")
-            hs = codes.tile([P, W], U8, align_bytes=64, name="hs")
+            hc = keep.tile([P, W], U32, align_bytes=64, name="hc")
+            hs = keep.tile([P, W], U8, align_bytes=64, name="hs")
             nc.vector.quantize_mx(
                 out=hc[:].bitcast(FP8X4), scales=hs[:], in_=gh_t[i][:].rearrange("p w t -> p (w t)")
             )
             hc_t[i] = (hc, hs)
 
-        def layer2(i):
+        def layer2(i, c):
             if live(i):
-                for c in [SER] + OTHERS:
-                    mx_pass((2, i, c), w2c, w2s, c, hc_t[i])
+                mx_pass((2, i, c), w2c, w2s, c, hc_t[i])
 
         def tanh_ser(i):
             if not live(i):
@@ -230,9 +269,13 @@ def tile_hebbianlayer_pb_t_kernel(
                 nc.tensor.transpose(bank[:, al, :], plane[:, al * P : (al + 1) * P], ident[:])
             ot_t[key] = bank
 
-        def mods(i, c):
+        def ser_mods(i):
             g, off = divmod(i * SCT, PAIR)
-            return mod_t[g][:, c, off : off + SCT, :]
+            return ms_t[g][:, off : off + SCT, :]
+
+        def other_mods(i, n):
+            g, off = divmod(i * SCT, PAIR)
+            return mo_t[g][:, n, off : off + SCT, :]
 
         def store(i, c, rows):
             nc.sync.dma_start(out=out_view[:, c, i * SCT : (i + 1) * SCT, :], in_=rows)
@@ -241,28 +284,27 @@ def tile_hebbianlayer_pb_t_kernel(
             if live(i):
                 back_to_rows((i, SER), ser_t[i])
 
-        def reciprocal_ser(i):
+        def square_ser(i):
             if not live(i):
                 return
-            inv = invp.tile([P, SCT, E], F32, name="inv")
-            nc.vector.reciprocal(out=inv[:], in_=ot_t[(i, SER)][:])
+            inv = keep.tile([P, SCT, E], F32, name="inv")
+            nc.scalar.activation(out=inv[:], in_=ot_t[(i, SER)][:], func=ACT.Square)
             inv_t[i] = inv
 
-        def abs_inv(i):
+        def inverse_ser(i):
             if live(i):
-                nc.scalar.activation(out=inv_t[i][:], in_=inv_t[i][:], func=ACT.Abs)
+                nc.scalar.activation(out=inv_t[i][:], in_=inv_t[i][:], func=ACT.Abs_reciprocal_sqrt)
 
         def exit_ser(i):
             if not live(i):
                 return
             res = sres.tile([P, SCT, E], F32, name="res")
-            nc.vector.tensor_tensor(out=res[:], in0=ot_t[(i, SER)][:], in1=mods(i, SER), op=ALU.add)
+            nc.vector.tensor_tensor(out=res[:], in0=ot_t[(i, SER)][:], in1=ser_mods(i), op=ALU.add)
             store(i, SER, res[:])
 
-        def transpose_others(i):
+        def transpose_back(i, n):
             if live(i):
-                for n in range(3):
-                    back_to_rows((i, n), ht_t[i][:, n, :])
+                back_to_rows((i, n), ht_t[i][:, n, :])
 
         def products(i, n):
             if not live(i):
@@ -283,34 +325,84 @@ def tile_hebbianlayer_pb_t_kernel(
             if not live(i):
                 return
             c = OTHERS[n]
-            nc.gpsimd.tensor_tensor(out=rs_t[i][:, n], in0=rs_t[i][:, n], in1=mods(i, c), op=ALU.add)
+            engine = nc.gpsimd if on_gpsimd(i, n) else nc.vector
+            engine.tensor_tensor(out=rs_t[i][:, n], in0=rs_t[i][:, n], in1=other_mods(i, n), op=ALU.add)
             store(i, c, rs_t[i][:, n])
 
-        for p in range(-2, NSC + 4):
-            if p % 2 == 0:
-                load_x((p + 4) // 2)
-                load_mods(p // 2)
-            for n in range(3):
-                products(p - 3, n)
-                add_mods(p - 3, n)
-            transpose_x(p + 1, 0)
-            transpose_x(p + 1, 1)
-            transpose_ser(p - 2)
+        def load_x_for(i):
+            g, off = divmod(i * SCT, PAIR)
+            if live(i) and off == 0:
+                load_x(g + 1)
+
+        def early_layer2(k):
+            if 0 <= k < 3 * EARLY:
+                layer2(k // 3, OTHERS[k % 3])
+
+        def early_tanh(k):
+            if 0 <= k < 3 * EARLY:
+                tanh(k // 3, k % 3)
+
+        for p in range(-3, NSC):
+            load_x_for(p + 2)
+            load_ser_mod((p + 1) // 2)
+            if p >= 4:
+                load_other_mods(min(MO_BUFS - 1, (p - 4) // 2))
             relu(p)
+            transpose_ser(p - 2)
             copy_x(p + 1, 0)
+            if p == -1:
+                regroup_w1(nc.vector.tensor_copy, 0)
+                regroup_w1(nc.scalar.copy, 1)
+                quantise_w1(0)
+                nc.vector.tensor_copy(out=b1t[:], in_=b1_bf[:])
             copy_x(p + 1, 1)
-            layer2(p - 1)
-            reciprocal_ser(p - 2)
+            layer2(p - 1, SER)
             exit_ser(p - 2)
+            square_ser(p - 2)
             tanh_ser(p - 1)
-            tanh(p - 1, 0)
-            abs_inv(p - 2)
-            tanh(p - 1, 1)
-            tanh(p - 1, 2)
+            early_layer2(p - EARLY_START)
+            early_tanh(p - EARLY_START)
+            if p == -1:
+                quantise_w1(1)
             quantise_x(p + 1)
+            transpose_x(p + 2, 0)
+            transpose_x(p + 2, 1)
             regroup_hid(p)
             quantise_hid(p)
-            transpose_others(p - 2)
             layer1(p + 1)
-            if p == -1:
+            if p == 0:
+                regroup_w2()
                 quantise_w2()
+        transpose_ser(NSC - 2)
+        exit_ser(NSC - 2)
+        layer2(NSC - 1, SER)
+        for k in range(NSC - EARLY_START, 3 * EARLY):
+            early_layer2(k)
+            early_tanh(k)
+        for i in range(NSC - 2):
+            inverse_ser(i)
+            if i == 2:
+                square_ser(NSC - 2)
+        inverse_ser(NSC - 2)
+        tanh_ser(NSC - 1)
+        for q in range(-1, NSC):
+            load_other_mods((q + 8) // 2)
+            for n in range(3):
+                products(q, n)
+            if q == LAST_SER:
+                exit_ser(NSC - 1)
+                square_ser(NSC - 1)
+            for n in range(3):
+                transpose_back(q + 1, n)
+            if q + 1 == LAST_SER:
+                transpose_ser(NSC - 1)
+            for n in range(3):
+                add_mods(q, n)
+            for n in range(3):
+                if q + AHEAD >= EARLY:
+                    layer2(q + AHEAD, OTHERS[n])
+            for n in range(3):
+                if q + AHEAD >= EARLY:
+                    tanh(q + AHEAD, n)
+            if q == LAST_INV:
+                inverse_ser(NSC - 1)

@@ -21,17 +21,17 @@ NSC = NT // SCT
 PAIR = 2 * SCT
 SER = 1
 OTHERS = [0, 2, 3]
-EARLY = 4
-EARLY_START = 3
-LAST_SER = 6
-LAST_INV = 10
+EARLY = 5
+EARLY_START = 1
+LAST_SER = 8
+LAST_INV = 12
 AHEAD = 3
 GW = 0
-MO_BUFS = 5
+MO_BUFS = 4
 
 
 def on_gpsimd(i, n):
-    return n < 2 and not (n == 1 and i % 4 == 3)
+    return n == 0 or (n == 1 and i < NSC - 1)
 
 
 def x_on_scalar(i, h):
@@ -56,14 +56,13 @@ def tile_hebbianlayer_pb_t_kernel(
         msp = ctx.enter_context(tc.tile_pool(name="msp", bufs=3))
         mop = ctx.enter_context(tc.tile_pool(name="mop", bufs=MO_BUFS))
         post = ctx.enter_context(tc.tile_pool(name="post", bufs=max(AHEAD + 1, EARLY) + 1))
-        resp = ctx.enter_context(tc.tile_pool(name="resp", bufs=3))
-        sres = ctx.enter_context(tc.tile_pool(name="sres", bufs=4))
+        resp = ctx.enter_context(tc.tile_pool(name="resp", bufs=12))
         ps_tp = ctx.enter_context(tc.psum_pool(name="ps_tp", bufs=4))
         ps_mm = ctx.enter_context(tc.psum_pool(name="ps_mm", bufs=4))
         ctx.enter_context(tc.manual_schedule())
 
         x_tiles, gx_t, xt_t, xc_t, mm_t, hidp_t, gh_t, hc_t = {}, {}, {}, {}, {}, {}, {}, {}
-        ser_t, inv_t, ht_t, ot_t, rs_t, ms_t, mo_t = {}, {}, {}, {}, {}, {}, {}
+        ser_t, inv_t, ht_t, ot_t, rs_t, ms_t, mo_t, mb_t = {}, {}, {}, {}, {}, {}, {}, {}
 
         def live(i):
             return 0 <= i < NSC
@@ -99,8 +98,16 @@ def tile_hebbianlayer_pb_t_kernel(
 
         ident = const.tile([P, P], F32)
         make_identity(nc, ident[:])
+        ident_bf = const.tile([P, P], BF16)
+        make_identity(nc, ident_bf[:])
+        b1_bf = const.tile([P, 4], BF16)
+        b2_bf = const.tile([P, 4], BF16)
+        nc.scalar.dma_start(out=b1_bf[:], in_=b1.rearrange("(m t) -> m t", t=4))
+        nc.scalar.dma_start(out=b2_bf[:], in_=b2.rearrange("(j c) -> j c", c=4))
         load_x(0)
         load_x_tiles(0, 0, 2)
+        warm = const.tile([P, 1], F32)
+        nc.scalar.activation(out=warm[:], in_=ident[:, 0:1], func=ACT.Tanh)
         raw1 = const.tile([P, 4, D], BF16)
         for u in range(2):
             nc.sync.dma_start(
@@ -108,10 +115,6 @@ def tile_hebbianlayer_pb_t_kernel(
                 in_=W1.rearrange("(q j) f -> q j f", j=4)[:, 2 * u : 2 * u + 2, :],
             )
         load_x_tiles(0, 2, 4)
-        b1_bf = const.tile([P, 4], BF16)
-        b2_bf = const.tile([P, 4], BF16)
-        nc.scalar.dma_start(out=b1_bf[:], in_=b1.rearrange("(m t) -> m t", t=4))
-        nc.scalar.dma_start(out=b2_bf[:], in_=b2.rearrange("(j c) -> j c", c=4))
         load_x_tiles(0, 4, 8)
         raw2 = const.tile([P, 4, D], BF16)
         nc.sync.dma_start(out=raw2[:], in_=W2.rearrange("(p t) n -> p t n", t=4))
@@ -298,7 +301,7 @@ def tile_hebbianlayer_pb_t_kernel(
         def exit_ser(i):
             if not live(i):
                 return
-            res = sres.tile([P, SCT, E], F32, name="res")
+            res = resp.tile([P, SCT, E], F32, name="res")
             nc.vector.tensor_tensor(out=res[:], in0=ot_t[(i, SER)][:], in1=ser_mods(i), op=ALU.add)
             store(i, SER, res[:])
 
@@ -309,11 +312,10 @@ def tile_hebbianlayer_pb_t_kernel(
         def products(i, n):
             if not live(i):
                 return
-            if i not in rs_t:
-                rs = resp.tile([P, 3, SCT, E], F32, name="rs")
-                rs_t[i] = rs
+            rs = resp.tile([P, SCT, E], F32, name="rs", tag="res")
+            rs_t[(i, n)] = rs
             nc.vector.scalar_tensor_tensor(
-                out=rs_t[i][:, n],
+                out=rs[:],
                 in0=inv_t[i][:],
                 scalar=1.0e6,
                 in1=ot_t[(i, n)][:],
@@ -321,13 +323,22 @@ def tile_hebbianlayer_pb_t_kernel(
                 op1=ALU.mult,
             )
 
+        def mods_to_psum(i, n):
+            if not live(i) or on_gpsimd(i, n):
+                return
+            bank = ps_tp.tile([P, SCT, E], F32, name="mb", tag="tp")
+            nc.tensor.matmul(out=bank[:], lhsT=ident_bf[:], rhs=other_mods(i, n), start=True, stop=True)
+            mb_t[(i, n)] = bank
+
         def add_mods(i, n):
             if not live(i):
                 return
             c = OTHERS[n]
-            engine = nc.gpsimd if on_gpsimd(i, n) else nc.vector
-            engine.tensor_tensor(out=rs_t[i][:, n], in0=rs_t[i][:, n], in1=other_mods(i, n), op=ALU.add)
-            store(i, c, rs_t[i][:, n])
+            if on_gpsimd(i, n):
+                nc.gpsimd.tensor_tensor(out=rs_t[(i, n)][:], in0=rs_t[(i, n)][:], in1=other_mods(i, n), op=ALU.add)
+            else:
+                nc.vector.tensor_tensor(out=rs_t[(i, n)][:], in0=mb_t[(i, n)][:], in1=rs_t[(i, n)][:], op=ALU.add)
+            store(i, c, rs_t[(i, n)][:])
 
         def load_x_for(i):
             g, off = divmod(i * SCT, PAIR)
@@ -349,7 +360,6 @@ def tile_hebbianlayer_pb_t_kernel(
                 load_other_mods(min(MO_BUFS - 1, (p - 4) // 2))
             relu(p)
             transpose_ser(p - 2)
-            copy_x(p + 1, 0)
             if p == -1:
                 regroup_w1(nc.vector.tensor_copy, 0)
                 regroup_w1(nc.scalar.copy, 1)
@@ -366,8 +376,9 @@ def tile_hebbianlayer_pb_t_kernel(
                 quantise_w1(1)
             quantise_x(p + 1)
             transpose_x(p + 2, 0)
-            transpose_x(p + 2, 1)
             regroup_hid(p)
+            copy_x(p + 2, 0)
+            transpose_x(p + 2, 1)
             quantise_hid(p)
             layer1(p + 1)
             if p == 0:
@@ -386,22 +397,22 @@ def tile_hebbianlayer_pb_t_kernel(
         inverse_ser(NSC - 2)
         tanh_ser(NSC - 1)
         for q in range(-1, NSC):
-            load_other_mods((q + 8) // 2)
-            for n in range(3):
+            load_other_mods((q + 6) // 2)
+            for n in (2, 1, 0):
                 products(q, n)
+                mods_to_psum(q, n)
+                transpose_back(q + 1, n)
             if q == LAST_SER:
                 exit_ser(NSC - 1)
                 square_ser(NSC - 1)
-            for n in range(3):
-                transpose_back(q + 1, n)
             if q + 1 == LAST_SER:
                 transpose_ser(NSC - 1)
-            for n in range(3):
+            for n in (2, 1, 0):
                 add_mods(q, n)
-            for n in range(3):
+            for n in (2, 1, 0):
                 if q + AHEAD >= EARLY:
                     layer2(q + AHEAD, OTHERS[n])
-            for n in range(3):
+            for n in (2, 1, 0):
                 if q + AHEAD >= EARLY:
                     tanh(q + AHEAD, n)
             if q == LAST_INV:

@@ -27,7 +27,7 @@ LAST_SER = 8
 LAST_INV = 12
 AHEAD = 3
 GW = 0
-MO_BUFS = 4
+MO_BUFS = 7
 
 
 def on_gpsimd(i, n):
@@ -108,7 +108,7 @@ def tile_hebbianlayer_pb_t_kernel(
         load_x_tiles(0, 0, 2)
         warm = const.tile([P, 1], F32)
         nc.scalar.activation(out=warm[:], in_=ident[:, 0:1], func=ACT.Tanh)
-        raw1 = const.tile([P, 4, D], BF16)
+        raw1 = work.tile([P, 4, D], BF16, name="raw1", tag="hidp")
         for u in range(2):
             nc.sync.dma_start(
                 out=raw1[:, 2 * u : 2 * u + 2, :],
@@ -116,16 +116,16 @@ def tile_hebbianlayer_pb_t_kernel(
             )
         load_x_tiles(0, 2, 4)
         load_x_tiles(0, 4, 8)
-        raw2 = const.tile([P, 4, D], BF16)
+        raw2 = work.tile([P, 4, D], BF16, name="raw2", tag="hidp")
         nc.sync.dma_start(out=raw2[:], in_=W2.rearrange("(p t) n -> p t n", t=4))
         load_x(1)
 
-        g1 = const.tile([P, D, 4], BF16, align_bytes=64)
+        g1 = work.tile([P, D, 4], BF16, align_bytes=64, name="g1", tag="gh")
         w1c = const.tile([P, D], U32, align_bytes=64)
         w1s = const.tile([P, D], U8, align_bytes=64)
         b1t = const.tile([P, 4], F32)
         b2t = const.tile([P, 4], F32)
-        g2 = const.tile([P, D, 4], BF16, align_bytes=64)
+        g2 = work.tile([P, D, 4], BF16, align_bytes=64, name="g2", tag="gh")
         w2c = const.tile([P, D], U32, align_bytes=64)
         w2s = const.tile([P, D], U8, align_bytes=64)
 
@@ -356,8 +356,7 @@ def tile_hebbianlayer_pb_t_kernel(
         for p in range(-3, NSC):
             load_x_for(p + 2)
             load_ser_mod((p + 1) // 2)
-            if p >= 4:
-                load_other_mods(min(MO_BUFS - 1, (p - 4) // 2))
+            load_other_mods(min(MO_BUFS - 1, p // 2))
             relu(p)
             transpose_ser(p - 2)
             if p == -1:
@@ -397,7 +396,7 @@ def tile_hebbianlayer_pb_t_kernel(
         inverse_ser(NSC - 2)
         tanh_ser(NSC - 1)
         for q in range(-1, NSC):
-            load_other_mods((q + 6) // 2)
+            load_other_mods((q + 2 * MO_BUFS - 2) // 2)
             for n in (2, 1, 0):
                 products(q, n)
                 mods_to_psum(q, n)

@@ -31,7 +31,7 @@ MO_BUFS = 7
 
 
 def on_gpsimd(i, n):
-    return n == 0 or (n == 1 and i < NSC - 1)
+    return n == 0 or (n == 1 and i % 2 == 0)
 
 
 def x_on_scalar(i, h):
@@ -326,7 +326,7 @@ def tile_hebbianlayer_pb_t_kernel(
         def mods_to_psum(i, n):
             if not live(i) or on_gpsimd(i, n):
                 return
-            bank = ps_tp.tile([P, SCT, E], F32, name="mb", tag="tp")
+            bank = ps_mm.tile([P, SCT, E], F32, name="mb", tag="mm")
             nc.tensor.matmul(out=bank[:], lhsT=ident_bf[:], rhs=other_mods(i, n), start=True, stop=True)
             mb_t[(i, n)] = bank
 
@@ -385,7 +385,6 @@ def tile_hebbianlayer_pb_t_kernel(
                 quantise_w2()
         transpose_ser(NSC - 2)
         exit_ser(NSC - 2)
-        layer2(NSC - 1, SER)
         for k in range(NSC - EARLY_START, 3 * EARLY):
             early_layer2(k)
             early_tanh(k)
@@ -394,25 +393,27 @@ def tile_hebbianlayer_pb_t_kernel(
             if i == 2:
                 square_ser(NSC - 2)
         inverse_ser(NSC - 2)
-        tanh_ser(NSC - 1)
         for q in range(-1, NSC):
             load_other_mods((q + 2 * MO_BUFS - 2) // 2)
             for n in (2, 1, 0):
                 products(q, n)
                 mods_to_psum(q, n)
                 transpose_back(q + 1, n)
+            for n in (2, 1, 0):
+                add_mods(q, n)
             if q == LAST_SER:
                 exit_ser(NSC - 1)
                 square_ser(NSC - 1)
             if q + 1 == LAST_SER:
                 transpose_ser(NSC - 1)
             for n in (2, 1, 0):
-                add_mods(q, n)
-            for n in (2, 1, 0):
                 if q + AHEAD >= EARLY:
                     layer2(q + AHEAD, OTHERS[n])
             for n in (2, 1, 0):
                 if q + AHEAD >= EARLY:
                     tanh(q + AHEAD, n)
+            if q == LAST_SER - 3:
+                layer2(NSC - 1, SER)
+                tanh_ser(NSC - 1)
             if q == LAST_INV:
                 inverse_ser(NSC - 1)

@@ -26,12 +26,19 @@ EARLY_START = 1
 LAST_SER = 8
 LAST_INV = 12
 AHEAD = 3
-GW = 0
 MO_BUFS = 7
 
 
 def on_gpsimd(i, n):
     return n == 0 or (n == 1 and i % 2 == 0)
+
+
+def gpsimd_columns(i):
+    return 128
+
+
+def relu_on_vector(i, t):
+    return False
 
 
 def x_on_scalar(i, h):
@@ -50,13 +57,14 @@ def tile_hebbianlayer_pb_t_kernel(
         const = ctx.enter_context(tc.tile_pool(name="const", bufs=1))
         xin = ctx.enter_context(tc.tile_pool(name="xin", bufs=2))
         work = ctx.enter_context(tc.tile_pool(name="work", bufs=2))
-        codes = ctx.enter_context(tc.tile_pool(name="codes", bufs=2))
+        ghp = ctx.enter_context(tc.tile_pool(name="ghp", bufs=1))
+        codes = ctx.enter_context(tc.tile_pool(name="codes", bufs=3))
         serp = ctx.enter_context(tc.tile_pool(name="serp", bufs=3))
         keep = ctx.enter_context(tc.tile_pool(name="keep", bufs=NSC))
         msp = ctx.enter_context(tc.tile_pool(name="msp", bufs=3))
         mop = ctx.enter_context(tc.tile_pool(name="mop", bufs=MO_BUFS))
         post = ctx.enter_context(tc.tile_pool(name="post", bufs=max(AHEAD + 1, EARLY) + 1))
-        resp = ctx.enter_context(tc.tile_pool(name="resp", bufs=12))
+        resp = ctx.enter_context(tc.tile_pool(name="resp", bufs=11))
         ps_tp = ctx.enter_context(tc.psum_pool(name="ps_tp", bufs=4))
         ps_mm = ctx.enter_context(tc.psum_pool(name="ps_mm", bufs=4))
         ctx.enter_context(tc.manual_schedule())
@@ -116,16 +124,16 @@ def tile_hebbianlayer_pb_t_kernel(
             )
         load_x_tiles(0, 2, 4)
         load_x_tiles(0, 4, 8)
-        raw2 = work.tile([P, 4, D], BF16, name="raw2", tag="hidp")
+        raw2 = post.tile([P, 4, D], BF16, name="raw2", tag="ht")
         nc.sync.dma_start(out=raw2[:], in_=W2.rearrange("(p t) n -> p t n", t=4))
         load_x(1)
 
-        g1 = work.tile([P, D, 4], BF16, align_bytes=64, name="g1", tag="gh")
+        g1 = work.tile([P, D, 4], BF16, align_bytes=64, name="g1", tag="gx")
         w1c = const.tile([P, D], U32, align_bytes=64)
         w1s = const.tile([P, D], U8, align_bytes=64)
         b1t = const.tile([P, 4], F32)
         b2t = const.tile([P, 4], F32)
-        g2 = work.tile([P, D, 4], BF16, align_bytes=64, name="g2", tag="gh")
+        g2 = const.tile([P, D, 4], BF16, align_bytes=64)
         w2c = const.tile([P, D], U32, align_bytes=64)
         w2s = const.tile([P, D], U8, align_bytes=64)
 
@@ -141,11 +149,13 @@ def tile_hebbianlayer_pb_t_kernel(
                 out=w1c[:, cols].bitcast(FP8X4), scales=w1s[:, cols], in_=g1[:, cols, :].rearrange("q c j -> q (c j)")
             )
 
-        def regroup_w2():
-            nc.scalar.copy(
-                out=g2[:].rearrange("q (c m) j -> q c m j", c=4),
-                in_=raw2[:].rearrange("q j (m c) -> q c m j", c=4),
-            )
+        def regroup_w2(c):
+            out = g2[:].rearrange("q (c m) j -> q c m j", c=4)[:, c]
+            src = raw2[:].rearrange("q j (m c) -> q c m j", c=4)[:, c]
+            if True:
+                nc.gpsimd.tensor_scalar(out=out, in0=src, scalar1=1.0, scalar2=0.0, op0=ALU.mult, op1=ALU.add)
+            else:
+                nc.scalar.copy(out=out, in_=src)
 
         def quantise_w2():
             nc.vector.tensor_copy(out=b2t[:], in_=b2_bf[:])
@@ -211,26 +221,42 @@ def tile_hebbianlayer_pb_t_kernel(
             hidp = work.tile([P, 4, W], BF16, name="hidp")
             hidp_t[i] = hidp
             for t in range(4):
+                if relu_on_vector(i, t):
+                    continue
                 nc.scalar.activation(
                     out=hidp[:, t, :], in_=mm_t[(1, i, t)][:], func=ACT.Relu, bias=b1t[:, t : t + 1], scale=1.0
                 )
 
+        def vector_relu(i):
+            if not live(i):
+                return
+            for t in range(4):
+                if relu_on_vector(i, t):
+                    nc.vector.tensor_scalar(
+                        out=hidp_t[i][:, t, :], in0=mm_t[(1, i, t)][:], scalar1=b1t[:, t : t + 1], scalar2=0.0,
+                        op0=ALU.add, op1=ALU.max,
+                    )
+
         def regroup_hid(i):
             if not live(i):
                 return
-            gh = work.tile([P, W, 4], BF16, align_bytes=64, name="gh")
+            gh = ghp.tile([P, W, 4], BF16, align_bytes=64, name="gh")
             gh_t[i] = gh
-            vw = W - (GW if 0 < i else 0)
-            nc.vector.tensor_copy(
-                out=gh[:, :vw].rearrange("p (c i) t -> p c t i", i=4),
-                in_=hidp_t[i][:, :, :vw].rearrange("p t (c i) -> p c t i", i=4),
-            )
-            if vw < W:
+            g = gpsimd_columns(i)
+            if g:
                 nc.gpsimd.tensor_scalar(
-                    out=gh[:, vw:].rearrange("p (c i) t -> p c t i", i=4),
-                    in0=hidp_t[i][:, :, vw:].rearrange("p t (c i) -> p c t i", i=4),
+                    out=gh[:, W - g :], in0=hidp_t[i][:, :, W - g :].rearrange("p t w -> p w t"),
                     scalar1=1.0, scalar2=0.0, op0=ALU.mult, op1=ALU.add,
                 )
+
+        def regroup_rest(i):
+            if not live(i):
+                return
+            v = W - gpsimd_columns(i)
+            nc.vector.tensor_copy(
+                out=gh_t[i][:, :v].rearrange("p (c i) t -> p c t i", i=4),
+                in_=hidp_t[i][:, :, :v].rearrange("p t (c i) -> p c t i", i=4),
+            )
 
         def quantise_hid(i):
             if not live(i):
@@ -353,36 +379,40 @@ def tile_hebbianlayer_pb_t_kernel(
             if 0 <= k < 3 * EARLY:
                 tanh(k // 3, k % 3)
 
-        for p in range(-3, NSC):
-            load_x_for(p + 2)
+        for p in range(-4, NSC):
+            load_x_for(p + 3)
+            if p == -1:
+                for c in range(4):
+                    regroup_w2(c)
+            regroup_hid(p)
             load_ser_mod((p + 1) // 2)
             load_other_mods(min(MO_BUFS - 1, p // 2))
-            relu(p)
-            transpose_ser(p - 2)
-            if p == -1:
+            copy_x(p + 2, 0)
+            if p == -2:
                 regroup_w1(nc.vector.tensor_copy, 0)
                 regroup_w1(nc.scalar.copy, 1)
                 quantise_w1(0)
                 nc.vector.tensor_copy(out=b1t[:], in_=b1_bf[:])
-            copy_x(p + 1, 1)
+            copy_x(p + 2, 1)
+            if p == 1:
+                quantise_w2()
+            relu(p + 1)
+            vector_relu(p + 1)
+            transpose_ser(p - 2)
             layer2(p - 1, SER)
-            exit_ser(p - 2)
-            square_ser(p - 2)
             tanh_ser(p - 1)
             early_layer2(p - EARLY_START)
             early_tanh(p - EARLY_START)
-            if p == -1:
+            transpose_x(p + 3, 0)
+            transpose_x(p + 3, 1)
+            if p == -2:
                 quantise_w1(1)
-            quantise_x(p + 1)
-            transpose_x(p + 2, 0)
-            regroup_hid(p)
-            copy_x(p + 2, 0)
-            transpose_x(p + 2, 1)
+            regroup_rest(p)
+            quantise_x(p + 2)
+            exit_ser(p - 2)
+            square_ser(p - 2)
             quantise_hid(p)
-            layer1(p + 1)
-            if p == 0:
-                regroup_w2()
-                quantise_w2()
+            layer1(p + 2)
         transpose_ser(NSC - 2)
         exit_ser(NSC - 2)
         for k in range(NSC - EARLY_START, 3 * EARLY):

@@ -30,7 +30,12 @@ MO_BUFS = 7
 
 
 def on_gpsimd(i, n):
-    return n == 0 or (n == 1 and i % 2 == 0)
+    return n == 0 or (n == 1 and (i % 3 != 0))
+
+
+def late_planes(q):
+    a = lambda r: min(3 * NSC, max(3 * EARLY, min(3 * (r + AHEAD + 1), 3 * EARLY + 1 + 4 * (r - 2))))
+    return range(a(q - 1), a(q))
 
 
 def gpsimd_columns(i):
@@ -42,7 +47,7 @@ def relu_on_vector(i, t):
 
 
 def x_on_scalar(i, h):
-    return False
+    return i == 0 and h == 1
 
 
 def tile_hebbianlayer_pb_t_kernel(
@@ -80,7 +85,7 @@ def tile_hebbianlayer_pb_t_kernel(
                 return
             xr = xin.tile([P, PAIR * D], BF16, name="xr")
             x_tiles[g] = xr
-            if g > 0:
+            if g > 1:
                 load_x_tiles(g, 0, PAIR)
 
         def load_x_tiles(g, a, b):
@@ -114,6 +119,7 @@ def tile_hebbianlayer_pb_t_kernel(
         nc.scalar.dma_start(out=b2_bf[:], in_=b2.rearrange("(j c) -> j c", c=4))
         load_x(0)
         load_x_tiles(0, 0, 2)
+        load_x_tiles(0, 2, 4)
         warm = const.tile([P, 1], F32)
         nc.scalar.activation(out=warm[:], in_=ident[:, 0:1], func=ACT.Tanh)
         raw1 = work.tile([P, 4, D], BF16, name="raw1", tag="hidp")
@@ -122,11 +128,12 @@ def tile_hebbianlayer_pb_t_kernel(
                 out=raw1[:, 2 * u : 2 * u + 2, :],
                 in_=W1.rearrange("(q j) f -> q j f", j=4)[:, 2 * u : 2 * u + 2, :],
             )
-        load_x_tiles(0, 2, 4)
         load_x_tiles(0, 4, 8)
+        load_x(1)
+        load_x_tiles(1, 0, 4)
         raw2 = post.tile([P, 4, D], BF16, name="raw2", tag="ht")
         nc.sync.dma_start(out=raw2[:], in_=W2.rearrange("(p t) n -> p t n", t=4))
-        load_x(1)
+        load_x_tiles(1, 4, 8)
 
         g1 = work.tile([P, D, 4], BF16, align_bytes=64, name="g1", tag="gx")
         w1c = const.tile([P, D], U32, align_bytes=64)
@@ -137,25 +144,23 @@ def tile_hebbianlayer_pb_t_kernel(
         w2c = const.tile([P, D], U32, align_bytes=64)
         w2s = const.tile([P, D], U8, align_bytes=64)
 
-        def regroup_w1(copy, half):
+        def regroup_w1(copy, t):
             copy(
-                out=g1[:].rearrange("q (t m) j -> q t m j", t=4)[:, 2 * half : 2 * half + 2],
-                in_=raw1[:].rearrange("q j (m t) -> q t m j", t=4)[:, 2 * half : 2 * half + 2],
+                out=g1[:].rearrange("q (t m) j -> q t m j", t=4)[:, t],
+                in_=raw1[:].rearrange("q j (m t) -> q t m j", t=4)[:, t],
             )
 
-        def quantise_w1(half):
-            cols = slice(half * D // 2, (half + 1) * D // 2)
+        def quantise_w1(a, b):
+            cols = slice(a * P, b * P)
             nc.vector.quantize_mx(
                 out=w1c[:, cols].bitcast(FP8X4), scales=w1s[:, cols], in_=g1[:, cols, :].rearrange("q c j -> q (c j)")
             )
 
-        def regroup_w2(c):
-            out = g2[:].rearrange("q (c m) j -> q c m j", c=4)[:, c]
-            src = raw2[:].rearrange("q j (m c) -> q c m j", c=4)[:, c]
-            if True:
-                nc.gpsimd.tensor_scalar(out=out, in0=src, scalar1=1.0, scalar2=0.0, op0=ALU.mult, op1=ALU.add)
-            else:
-                nc.scalar.copy(out=out, in_=src)
+        def regroup_w2():
+            nc.vector.tensor_copy(
+                out=g2[:].rearrange("q (c m) j -> q c m j", c=4),
+                in_=raw2[:].rearrange("q j (m c) -> q c m j", c=4),
+            )
 
         def quantise_w2():
             nc.vector.tensor_copy(out=b2t[:], in_=b2_bf[:])
@@ -381,36 +386,44 @@ def tile_hebbianlayer_pb_t_kernel(
 
         for p in range(-4, NSC):
             load_x_for(p + 3)
-            if p == -1:
-                for c in range(4):
-                    regroup_w2(c)
+            if p == 0:
+                regroup_w2()
             regroup_hid(p)
             load_ser_mod((p + 1) // 2)
             load_other_mods(min(MO_BUFS - 1, p // 2))
             copy_x(p + 2, 0)
             if p == -2:
                 regroup_w1(nc.vector.tensor_copy, 0)
-                regroup_w1(nc.scalar.copy, 1)
-                quantise_w1(0)
+                quantise_w1(0, 1)
                 nc.vector.tensor_copy(out=b1t[:], in_=b1_bf[:])
             copy_x(p + 2, 1)
+            if p == -2:
+                regroup_w1(nc.scalar.copy, 2)
+                regroup_w1(nc.scalar.copy, 3)
+                quantise_x(0)
+                regroup_w1(nc.vector.tensor_copy, 1)
+                quantise_w1(1, 2)
+                quantise_w1(2, 4)
             if p == 1:
                 quantise_w2()
             relu(p + 1)
             vector_relu(p + 1)
-            transpose_ser(p - 2)
+            if p < NSC - 1:
+                transpose_ser(p - 2)
             layer2(p - 1, SER)
             tanh_ser(p - 1)
+            if p == NSC - 1:
+                transpose_ser(p - 2)
             early_layer2(p - EARLY_START)
             early_tanh(p - EARLY_START)
             transpose_x(p + 3, 0)
             transpose_x(p + 3, 1)
-            if p == -2:
-                quantise_w1(1)
             regroup_rest(p)
-            quantise_x(p + 2)
+            if p > -2:
+                quantise_x(p + 2)
             exit_ser(p - 2)
-            square_ser(p - 2)
+            if p < NSC - 1:
+                square_ser(p - 2)
             quantise_hid(p)
             layer1(p + 2)
         transpose_ser(NSC - 2)
@@ -418,11 +431,12 @@ def tile_hebbianlayer_pb_t_kernel(
         for k in range(NSC - EARLY_START, 3 * EARLY):
             early_layer2(k)
             early_tanh(k)
-        for i in range(NSC - 2):
+        for i in range(15):
             inverse_ser(i)
-            if i == 2:
+            if i == 0:
+                square_ser(NSC - 3)
+            if i == 1:
                 square_ser(NSC - 2)
-        inverse_ser(NSC - 2)
         for q in range(-1, NSC):
             load_other_mods((q + 2 * MO_BUFS - 2) // 2)
             for n in (2, 1, 0):
@@ -436,14 +450,14 @@ def tile_hebbianlayer_pb_t_kernel(
                 square_ser(NSC - 1)
             if q + 1 == LAST_SER:
                 transpose_ser(NSC - 1)
-            for n in (2, 1, 0):
-                if q + AHEAD >= EARLY:
-                    layer2(q + AHEAD, OTHERS[n])
-            for n in (2, 1, 0):
-                if q + AHEAD >= EARLY:
-                    tanh(q + AHEAD, n)
+            planes = late_planes(q)
+            for k in planes:
+                layer2(k // 3, OTHERS[2 - k % 3])
+            for k in planes:
+                tanh(k // 3, 2 - k % 3)
             if q == LAST_SER - 3:
                 layer2(NSC - 1, SER)
                 tanh_ser(NSC - 1)
             if q == LAST_INV:
-                inverse_ser(NSC - 1)
+                for i in range(15, NSC):
+                    inverse_ser(i)

@@ -30,7 +30,7 @@ MO_BUFS = 7
 
 
 def on_gpsimd(i, n):
-    return n == 0 or (n == 1 and (i % 3 != 0))
+    return i < NSC - 1 and (n == 0 or (n == 1 and (i < 5 or i % 4 != 3)))
 
 
 def late_planes(q):
@@ -43,11 +43,11 @@ def gpsimd_columns(i):
 
 
 def relu_on_vector(i, t):
-    return False
+    return i == NSC - 1 and t == 3
 
 
 def x_on_scalar(i, h):
-    return i == 0 and h == 1
+    return i in (0, 2) and h == 1
 
 
 def tile_hebbianlayer_pb_t_kernel(
@@ -311,8 +311,8 @@ def tile_hebbianlayer_pb_t_kernel(
             g, off = divmod(i * SCT, PAIR)
             return mo_t[g][:, n, off : off + SCT, :]
 
-        def store(i, c, rows):
-            nc.sync.dma_start(out=out_view[:, c, i * SCT : (i + 1) * SCT, :], in_=rows)
+        def store(i, c, rows, queue=nc.sync):
+            queue.dma_start(out=out_view[:, c, i * SCT : (i + 1) * SCT, :], in_=rows)
 
         def transpose_ser(i):
             if live(i):
@@ -357,7 +357,10 @@ def tile_hebbianlayer_pb_t_kernel(
         def mods_to_psum(i, n):
             if not live(i) or on_gpsimd(i, n):
                 return
-            bank = ps_mm.tile([P, SCT, E], F32, name="mb", tag="mm")
+            if 3 <= i <= 6:
+                bank = ps_tp.tile([P, SCT, E], F32, name="mb", tag="tp")
+            else:
+                bank = ps_mm.tile([P, SCT, E], F32, name="mb", tag="mm")
             nc.tensor.matmul(out=bank[:], lhsT=ident_bf[:], rhs=other_mods(i, n), start=True, stop=True)
             mb_t[(i, n)] = bank
 
@@ -369,7 +372,8 @@ def tile_hebbianlayer_pb_t_kernel(
                 nc.gpsimd.tensor_tensor(out=rs_t[(i, n)][:], in0=rs_t[(i, n)][:], in1=other_mods(i, n), op=ALU.add)
             else:
                 nc.vector.tensor_tensor(out=rs_t[(i, n)][:], in0=mb_t[(i, n)][:], in1=rs_t[(i, n)][:], op=ALU.add)
-            store(i, c, rs_t[(i, n)][:])
+            late = on_gpsimd(i, n) and i >= 13
+            store(i, c, rs_t[(i, n)][:], nc.scalar if late else nc.sync)
 
         def load_x_for(i):
             g, off = divmod(i * SCT, PAIR)
@@ -394,20 +398,18 @@ def tile_hebbianlayer_pb_t_kernel(
             copy_x(p + 2, 0)
             if p == -2:
                 regroup_w1(nc.vector.tensor_copy, 0)
-                quantise_w1(0, 1)
+                regroup_w1(nc.vector.tensor_copy, 1)
                 nc.vector.tensor_copy(out=b1t[:], in_=b1_bf[:])
+                quantise_w1(0, 2)
             copy_x(p + 2, 1)
             if p == -2:
                 regroup_w1(nc.scalar.copy, 2)
                 regroup_w1(nc.scalar.copy, 3)
                 quantise_x(0)
-                regroup_w1(nc.vector.tensor_copy, 1)
-                quantise_w1(1, 2)
                 quantise_w1(2, 4)
             if p == 1:
                 quantise_w2()
             relu(p + 1)
-            vector_relu(p + 1)
             if p < NSC - 1:
                 transpose_ser(p - 2)
             layer2(p - 1, SER)
@@ -425,6 +427,7 @@ def tile_hebbianlayer_pb_t_kernel(
             if p < NSC - 1:
                 square_ser(p - 2)
             quantise_hid(p)
+            vector_relu(p + 1)
             layer1(p + 2)
         transpose_ser(NSC - 2)
         exit_ser(NSC - 2)
@@ -441,10 +444,14 @@ def tile_hebbianlayer_pb_t_kernel(
             load_other_mods((q + 2 * MO_BUFS - 2) // 2)
             for n in (2, 1, 0):
                 products(q, n)
-                mods_to_psum(q, n)
+                if not 3 <= q <= 6:
+                    mods_to_psum(q, n)
                 transpose_back(q + 1, n)
             for n in (2, 1, 0):
                 add_mods(q, n)
+            for n in (2, 1, 0):
+                if 3 <= q + 1 <= 6:
+                    mods_to_psum(q + 1, n)
             if q == LAST_SER:
                 exit_ser(NSC - 1)
                 square_ser(NSC - 1)

from contextlib import ExitStack

import concourse.mybir as mybir
from concourse.masks import make_identity

F32 = mybir.dt.float32
BF16 = mybir.dt.bfloat16
U32 = mybir.dt.uint32
U8 = mybir.dt.uint8
FP8X4 = mybir.dt.float8_e4m3fn_x4
ACT = mybir.ActivationFunctionType
ALU = mybir.AluOpType

P = 128
B, D, E, NM = 8192, 512, 128, 4
FLOPS = 2 * B * D * D + 2 * B * D * NM * E
NT = B // P
SCT = 4
W = SCT * P
NSC = NT // SCT
PAIR = 2 * SCT
SER = 1
OTHERS = [0, 2, 3]
EARLY = 5
EARLY_START = 1
LAST_SER = 8
LAST_INV = 12
AHEAD = 3
MO_BUFS = 7


def on_gpsimd(i, n):
    return i < NSC - 1 and (n == 0 or (n == 1 and (i < 5 or i % 4 != 3)))


def late_planes(q):
    a = lambda r: min(3 * NSC, max(3 * EARLY, min(3 * (r + AHEAD + 1), 3 * EARLY + 1 + 4 * (r - 2))))
    return range(a(q - 1), a(q))


def gpsimd_columns(i):
    return 128


def relu_on_vector(i, t):
    return i == NSC - 1 and t == 3


def x_on_scalar(i, h):
    return i in (0, 2) and h == 1


def tile_hebbianlayer_pb_t_kernel(
    tc, prev_act, W1, b1, W2, b2, dopamine, serotonin, glutamate, gaba, out
):
    nc = tc.nc
    x_view = prev_act.rearrange("(p a) k -> p (a k)", a=NT)
    mod_views = [m.rearrange("(p a) j -> p a j", a=NT) for m in (dopamine, serotonin, glutamate, gaba)]
    out_view = out.rearrange("(c p a) j -> p c a j", c=NM, p=P, a=NT)

    with ExitStack() as ctx:
        const = ctx.enter_context(tc.tile_pool(name="const", bufs=1))
        xin = ctx.enter_context(tc.tile_pool(name="xin", bufs=2))
        work = ctx.enter_context(tc.tile_pool(name="work", bufs=2))
        ghp = ctx.enter_context(tc.tile_pool(name="ghp", bufs=1))
        codes = ctx.enter_context(tc.tile_pool(name="codes", bufs=3))
        serp = ctx.enter_context(tc.tile_pool(name="serp", bufs=3))
        keep = ctx.enter_context(tc.tile_pool(name="keep", bufs=NSC))
        msp = ctx.enter_context(tc.tile_pool(name="msp", bufs=3))
        mop = ctx.enter_context(tc.tile_pool(name="mop", bufs=MO_BUFS))
        post = ctx.enter_context(tc.tile_pool(name="post", bufs=max(AHEAD + 1, EARLY) + 1))
        resp = ctx.enter_context(tc.tile_pool(name="resp", bufs=11))
        ps_tp = ctx.enter_context(tc.psum_pool(name="ps_tp", bufs=4))
        ps_mm = ctx.enter_context(tc.psum_pool(name="ps_mm", bufs=4))
        ctx.enter_context(tc.manual_schedule())

        x_tiles, gx_t, xt_t, xc_t, mm_t, hidp_t, gh_t, hc_t = {}, {}, {}, {}, {}, {}, {}, {}
        ser_t, inv_t, ht_t, ot_t, rs_t, ms_t, mo_t, mb_t = {}, {}, {}, {}, {}, {}, {}, {}

        def live(i):
            return 0 <= i < NSC

        def load_x(g):
            if g * PAIR >= NT or g in x_tiles:
                return
            xr = xin.tile([P, PAIR * D], BF16, name="xr")
            x_tiles[g] = xr
            if g > 1:
                load_x_tiles(g, 0, PAIR)

        def load_x_tiles(g, a, b):
            nc.sync.dma_start(
                out=x_tiles[g][:, a * D : b * D],
                in_=x_view[:, (g * PAIR + a) * D : (g * PAIR + b) * D],
            )

        def load_ser_mod(g):
            if g < 0 or g * PAIR >= NT or g in ms_t:
                return
            ms = msp.tile([P, PAIR, E], BF16, name="ms")
            nc.sync.dma_start(out=ms[:], in_=mod_views[SER][:, g * PAIR : (g + 1) * PAIR, :])
            ms_t[g] = ms

        def load_other_mods(g):
            if g < 0 or g * PAIR >= NT or g in mo_t:
                return
            mo = mop.tile([P, 3, PAIR, E], BF16, name="mo")
            for n in range(3):
                nc.sync.dma_start(out=mo[:, n, :, :], in_=mod_views[OTHERS[n]][:, g * PAIR : (g + 1) * PAIR, :])
            mo_t[g] = mo

        ident = const.tile([P, P], F32)
        make_identity(nc, ident[:])
        ident_bf = const.tile([P, P], BF16)
        make_identity(nc, ident_bf[:])
        b1_bf = const.tile([P, 4], BF16)
        b2_bf = const.tile([P, 4], BF16)
        nc.scalar.dma_start(out=b1_bf[:], in_=b1.rearrange("(m t) -> m t", t=4))
        nc.scalar.dma_start(out=b2_bf[:], in_=b2.rearrange("(j c) -> j c", c=4))
        load_x(0)
        load_x_tiles(0, 0, 2)
        load_x_tiles(0, 2, 4)
        warm = const.tile([P, 1], F32)
        nc.scalar.activation(out=warm[:], in_=ident[:, 0:1], func=ACT.Tanh)
        raw1 = work.tile([P, 4, D], BF16, name="raw1", tag="hidp")
        for u in range(2):
            nc.sync.dma_start(
                out=raw1[:, 2 * u : 2 * u + 2, :],
                in_=W1.rearrange("(q j) f -> q j f", j=4)[:, 2 * u : 2 * u + 2, :],
            )
        load_x_tiles(0, 4, 8)
        load_x(1)
        load_x_tiles(1, 0, 4)
        raw2 = post.tile([P, 4, D], BF16, name="raw2", tag="ht")
        nc.sync.dma_start(out=raw2[:], in_=W2.rearrange("(p t) n -> p t n", t=4))
        load_x_tiles(1, 4, 8)

        g1 = work.tile([P, D, 4], BF16, align_bytes=64, name="g1", tag="gx")
        w1c = const.tile([P, D], U32, align_bytes=64)
        w1s = const.tile([P, D], U8, align_bytes=64)
        b1t = const.tile([P, 4], F32)
        b2t = const.tile([P, 4], F32)
        g2 = const.tile([P, D, 4], BF16, align_bytes=64)
        w2c = const.tile([P, D], U32, align_bytes=64)
        w2s = const.tile([P, D], U8, align_bytes=64)

        def regroup_w1(copy, t):
            copy(
                out=g1[:].rearrange("q (t m) j -> q t m j", t=4)[:, t],
                in_=raw1[:].rearrange("q j (m t) -> q t m j", t=4)[:, t],
            )

        def quantise_w1(a, b):
            cols = slice(a * P, b * P)
            nc.vector.quantize_mx(
                out=w1c[:, cols].bitcast(FP8X4), scales=w1s[:, cols], in_=g1[:, cols, :].rearrange("q c j -> q (c j)")
            )

        def regroup_w2():
            nc.vector.tensor_copy(
                out=g2[:].rearrange("q (c m) j -> q c m j", c=4),
                in_=raw2[:].rearrange("q j (m c) -> q c m j", c=4),
            )

        def quantise_w2():
            nc.vector.tensor_copy(out=b2t[:], in_=b2_bf[:])
            nc.vector.quantize_mx(
                out=w2c[:].bitcast(FP8X4), scales=w2s[:], in_=g2[:].rearrange("q c j -> q (c j)")
            )

        def transpose_x(i, h):
            if not live(i):
                return
            g, off = divmod(i * SCT, PAIR)
            x32 = x_tiles[g][:].bitcast(F32)
            xt = ps_tp.tile([P, 2, 2, P], F32, name="xt", tag="tp")
            for al in range(2):
                for u in range(2):
                    col = (off + 2 * h + al) * 256
                    nc.tensor.transpose(xt[:, al, u, :], x32[:, col + u : col + 256 : 2], ident[:])
            xt_t[(i, h)] = xt

        def copy_x(i, h):
            if not live(i):
                return
            if i not in gx_t:
                gx = work.tile([P, 4 * W], BF16, align_bytes=64, name="gx")
                gx_t[i] = gx
            gx32 = gx_t[i][:].bitcast(F32).rearrange("q (a b u) -> q a b u", a=SCT, u=2)
            o = gx32[:, 2 * h : 2 * h + 2]
            src = xt_t[(i, h)][:].rearrange("q a u b -> q a b u")
            if x_on_scalar(i, h):
                nc.scalar.copy(out=o, in_=src)
            else:
                nc.vector.tensor_copy(out=o, in_=src)

        def quantise_x(i):
            if not live(i):
                return
            xc = codes.tile([P, W], U32, align_bytes=64, name="xc")
            xs = codes.tile([P, W], U8, align_bytes=64, name="xs")
            nc.vector.quantize_mx(out=xc[:].bitcast(FP8X4), scales=xs[:], in_=gx_t[i][:])
            xc_t[i] = (xc, xs)

        def mx_pass(key, wc, ws, col, operand):
            acc = ps_mm.tile([P, W], F32, name="mm")
            nc.tensor.matmul_mx(
                out=acc[:],
                lhsT=wc[:, col * P : (col + 1) * P].bitcast(FP8X4),
                lhsT_scale=ws[:, col * P : (col + 1) * P],
                rhs=operand[0][:].bitcast(FP8X4),
                rhs_scale=operand[1][:],
                start=True,
                stop=True,
            )
            mm_t[key] = acc

        def layer1(i):
            if live(i):
                for t in range(4):
                    mx_pass((1, i, t), w1c, w1s, t, xc_t[i])

        def relu(i):
            if not live(i):
                return
            hidp = work.tile([P, 4, W], BF16, name="hidp")
            hidp_t[i] = hidp
            for t in range(4):
                if relu_on_vector(i, t):
                    continue
                nc.scalar.activation(
                    out=hidp[:, t, :], in_=mm_t[(1, i, t)][:], func=ACT.Relu, bias=b1t[:, t : t + 1], scale=1.0
                )

        def vector_relu(i):
            if not live(i):
                return
            for t in range(4):
                if relu_on_vector(i, t):
                    nc.vector.tensor_scalar(
                        out=hidp_t[i][:, t, :], in0=mm_t[(1, i, t)][:], scalar1=b1t[:, t : t + 1], scalar2=0.0,
                        op0=ALU.add, op1=ALU.max,
                    )

        def regroup_hid(i):
            if not live(i):
                return
            gh = ghp.tile([P, W, 4], BF16, align_bytes=64, name="gh")
            gh_t[i] = gh
            g = gpsimd_columns(i)
            if g:
                nc.gpsimd.tensor_scalar(
                    out=gh[:, W - g :], in0=hidp_t[i][:, :, W - g :].rearrange("p t w -> p w t"),
                    scalar1=1.0, scalar2=0.0, op0=ALU.mult, op1=ALU.add,
                )

        def regroup_rest(i):
            if not live(i):
                return
            v = W - gpsimd_columns(i)
            nc.vector.tensor_copy(
                out=gh_t[i][:, :v].rearrange("p (c i) t -> p c t i", i=4),
                in_=hidp_t[i][:, :, :v].rearrange("p t (c i) -> p c t i", i=4),
            )

        def quantise_hid(i):
            if not live(i):
                return
            hc = keep.tile([P, W], U32, align_bytes=64, name="hc")
            hs = keep.tile([P, W], U8, align_bytes=64, name="hs")
            nc.vector.quantize_mx(
                out=hc[:].bitcast(FP8X4), scales=hs[:], in_=gh_t[i][:].rearrange("p w t -> p (w t)")
            )
            hc_t[i] = (hc, hs)

        def layer2(i, c):
            if live(i):
                mx_pass((2, i, c), w2c, w2s, c, hc_t[i])

        def tanh_ser(i):
            if not live(i):
                return
            ser = serp.tile([P, W], F32, name="ser")
            nc.scalar.activation(
                out=ser[:], in_=mm_t[(2, i, SER)][:], func=ACT.Tanh, bias=b2t[:, SER : SER + 1], scale=1.0
            )
            ser_t[i] = ser

        def tanh(i, n):
            if not live(i):
                return
            if i not in ht_t:
                ht = post.tile([P, 3, W], F32, name="ht")
                ht_t[i] = ht
            c = OTHERS[n]
            nc.scalar.activation(
                out=ht_t[i][:, n, :], in_=mm_t[(2, i, c)][:], func=ACT.Tanh, bias=b2t[:, c : c + 1], scale=1.0
            )

        def back_to_rows(key, plane):
            bank = ps_tp.tile([P, SCT, E], F32, name="ot", tag="tp")
            for al in range(SCT):
                nc.tensor.transpose(bank[:, al, :], plane[:, al * P : (al + 1) * P], ident[:])
            ot_t[key] = bank

        def ser_mods(i):
            g, off = divmod(i * SCT, PAIR)
            return ms_t[g][:, off : off + SCT, :]

        def other_mods(i, n):
            g, off = divmod(i * SCT, PAIR)
            return mo_t[g][:, n, off : off + SCT, :]

        def store(i, c, rows, queue=nc.sync):
            queue.dma_start(out=out_view[:, c, i * SCT : (i + 1) * SCT, :], in_=rows)

        def transpose_ser(i):
            if live(i):
                back_to_rows((i, SER), ser_t[i])

        def square_ser(i):
            if not live(i):
                return
            inv = keep.tile([P, SCT, E], F32, name="inv")
            nc.scalar.activation(out=inv[:], in_=ot_t[(i, SER)][:], func=ACT.Square)
            inv_t[i] = inv

        def inverse_ser(i):
            if live(i):
                nc.scalar.activation(out=inv_t[i][:], in_=inv_t[i][:], func=ACT.Abs_reciprocal_sqrt)

        def exit_ser(i):
            if not live(i):
                return
            res = resp.tile([P, SCT, E], F32, name="res")
            nc.vector.tensor_tensor(out=res[:], in0=ot_t[(i, SER)][:], in1=ser_mods(i), op=ALU.add)
            store(i, SER, res[:])

        def transpose_back(i, n):
            if live(i):
                back_to_rows((i, n), ht_t[i][:, n, :])

        def products(i, n):
            if not live(i):
                return
            rs = resp.tile([P, SCT, E], F32, name="rs", tag="res")
            rs_t[(i, n)] = rs
            nc.vector.scalar_tensor_tensor(
                out=rs[:],
                in0=inv_t[i][:],
                scalar=1.0e6,
                in1=ot_t[(i, n)][:],
                op0=ALU.min,
                op1=ALU.mult,
            )

        def mods_to_psum(i, n):
            if not live(i) or on_gpsimd(i, n):
                return
            if 3 <= i <= 6:
                bank = ps_tp.tile([P, SCT, E], F32, name="mb", tag="tp")
            else:
                bank = ps_mm.tile([P, SCT, E], F32, name="mb", tag="mm")
            nc.tensor.matmul(out=bank[:], lhsT=ident_bf[:], rhs=other_mods(i, n), start=True, stop=True)
            mb_t[(i, n)] = bank

        def add_mods(i, n):
            if not live(i):
                return
            c = OTHERS[n]
            if on_gpsimd(i, n):
                nc.gpsimd.tensor_tensor(out=rs_t[(i, n)][:], in0=rs_t[(i, n)][:], in1=other_mods(i, n), op=ALU.add)
            else:
                nc.vector.tensor_tensor(out=rs_t[(i, n)][:], in0=mb_t[(i, n)][:], in1=rs_t[(i, n)][:], op=ALU.add)
            late = on_gpsimd(i, n) and i >= 13
            store(i, c, rs_t[(i, n)][:], nc.scalar if late else nc.sync)

        def load_x_for(i):
            g, off = divmod(i * SCT, PAIR)
            if live(i) and off == 0:
                load_x(g + 1)

        def early_layer2(k):
            if 0 <= k < 3 * EARLY:
                layer2(k // 3, OTHERS[k % 3])

        def early_tanh(k):
            if 0 <= k < 3 * EARLY:
                tanh(k // 3, k % 3)

        for p in range(-4, NSC):
            load_x_for(p + 3)
            if p == 0:
                regroup_w2()
            regroup_hid(p)
            load_ser_mod((p + 1) // 2)
            load_other_mods(min(MO_BUFS - 1, p // 2))
            copy_x(p + 2, 0)
            if p == -2:
                regroup_w1(nc.vector.tensor_copy, 0)
                regroup_w1(nc.vector.tensor_copy, 1)
                nc.vector.tensor_copy(out=b1t[:], in_=b1_bf[:])
                quantise_w1(0, 2)
            copy_x(p + 2, 1)
            if p == -2:
                regroup_w1(nc.scalar.copy, 2)
                regroup_w1(nc.scalar.copy, 3)
                quantise_x(0)
                quantise_w1(2, 4)
            if p == 1:
                quantise_w2()
            relu(p + 1)
            if p < NSC - 1:
                transpose_ser(p - 2)
            layer2(p - 1, SER)
            tanh_ser(p - 1)
            if p == NSC - 1:
                transpose_ser(p - 2)
            early_layer2(p - EARLY_START)
            early_tanh(p - EARLY_START)
            transpose_x(p + 3, 0)
            transpose_x(p + 3, 1)
            regroup_rest(p)
            if p > -2:
                quantise_x(p + 2)
            exit_ser(p - 2)
            if p < NSC - 1:
                square_ser(p - 2)
            quantise_hid(p)
            vector_relu(p + 1)
            layer1(p + 2)
        transpose_ser(NSC - 2)
        exit_ser(NSC - 2)
        for k in range(NSC - EARLY_START, 3 * EARLY):
            early_layer2(k)
            early_tanh(k)
        for i in range(15):
            inverse_ser(i)
            if i == 0:
                square_ser(NSC - 3)
            if i == 1:
                square_ser(NSC - 2)
        for q in range(-1, NSC):
            load_other_mods((q + 2 * MO_BUFS - 2) // 2)
            for n in (2, 1, 0):
                products(q, n)
                if not 3 <= q <= 6:
                    mods_to_psum(q, n)
                transpose_back(q + 1, n)
            for n in (2, 1, 0):
                add_mods(q, n)
            for n in (2, 1, 0):
                if 3 <= q + 1 <= 6:
                    mods_to_psum(q + 1, n)
            if q == LAST_SER:
                exit_ser(NSC - 1)
                square_ser(NSC - 1)
            if q + 1 == LAST_SER:
                transpose_ser(NSC - 1)
            planes = late_planes(q)
            for k in planes:
                layer2(k // 3, OTHERS[2 - k % 3])
            for k in planes:
                tanh(k // 3, 2 - k % 3)
            if q == LAST_SER - 3:
                layer2(NSC - 1, SER)
                tanh_ser(NSC - 1)
            if q == LAST_INV:
                for i in range(15, NSC):
                    inverse_ser(i)
